import numpy as np
import ml_dtypes


def mxq(x, axis, fmt="e4m3"):
    dtype, down = {"e4m3": (ml_dtypes.float8_e4m3fn, 7), "e5m2": (ml_dtypes.float8_e5m2, 14)}[fmt]
    v = np.moveaxis(np.asarray(x, np.float32).astype(ml_dtypes.bfloat16).astype(np.float64), axis, -1)
    blocks = v.reshape(v.shape[:-1] + (-1, 32))
    amax = np.abs(blocks).max(-1, keepdims=True)
    byte = np.maximum(np.where(amax > 0, np.frexp(amax)[1] - 1 + 127, 0) - down, 1)
    scale = np.exp2(byte - 127.0)
    codes = (blocks / scale).astype(np.float32).astype(dtype).astype(np.float64)
    return np.moveaxis((codes * scale).reshape(v.shape), -1, axis)


WIDE = False


def mx_kscale(k):
    if not WIDE:
        return np.ones(k)
    levels = np.array([10, -10, 5, -5, 0])
    a = np.random.permutation(np.resize(levels, k // 512 * 4)).reshape(k // 512, 4)
    idx = np.arange(k)
    return np.exp2(a[idx // 512, idx % 128 // 32])


BF16 = ml_dtypes.bfloat16


def bf(x):
    return np.asarray(x, np.float32).astype(BF16)


def f64(x):
    return np.asarray(x).astype(np.float64)


E2M1 = np.array([0.0, 0.5, 1.0, 1.5, 2.0, 3.0, 4.0, 6.0, -0.0, -0.5, -1.0, -1.5, -2.0, -3.0, -4.0, -6.0])


def pack_weight(w, fmt):
    k, n = w.shape
    w = f64(bf(w)).reshape(k // 32, 32, n)
    amax = np.abs(w).max(1)
    if fmt == "e4m3":
        byte = np.frexp(amax)[1] - 1 + 127 - 7
    else:
        mant, ex = np.frexp(amax / 6.0)
        byte = np.where(mant > 0.5, ex, ex - 1) + 127
    byte = np.clip(np.where(amax > 0, byte, 1), 1, 254)
    scaled = (w * np.exp2(127.0 - byte)[:, None, :]).reshape(k, n).astype(np.float32)
    by_word = np.ascontiguousarray(scaled.reshape(k // 512, 128, 4, n).transpose(0, 1, 3, 2))
    if fmt == "e4m3":
        words = by_word.astype(ml_dtypes.float8_e4m3fn).view(np.uint8)
    else:
        c = by_word.astype(ml_dtypes.float4_e2m1fn).view(np.uint8) & 0xF
        words = c[..., 0::2] | (c[..., 1::2] << 4)
    return np.ascontiguousarray(words), np.ascontiguousarray(byte.astype(np.uint8).reshape(k // 512, 16, n))


def unpack_weight(words, scales, fmt):
    g, p, n, _ = words.shape
    if fmt == "e4m3":
        vals = np.ascontiguousarray(words).view(ml_dtypes.float8_e4m3fn).astype(np.float64)
    else:
        nib = np.empty((g, p, n, 4), np.uint8)
        nib[..., 0::2] = words & 0xF
        nib[..., 1::2] = words >> 4
        vals = E2M1[nib]
    vals = vals * np.repeat(np.exp2(scales.astype(np.float64) - 127.0), 8, axis=1)[..., None]
    return vals.transpose(0, 1, 3, 2).reshape(g * 512, n)


B, T, U, H = 4, 64, 32, 512
INNER, VOCAB = 512, 1024
FMT = "e4m3"


def log_softmax(v):
    sh = v - v.max(-1, keepdims=True)
    return sh - np.log(np.exp(sh).sum(-1, keepdims=True))


def setup_inputs():
    s = mx_kscale(2 * H)
    enc_state = bf(np.random.standard_normal((B, T, H)) * s[:H])
    dec_state = bf(np.random.standard_normal((B, U, H)) * s[H:])
    W1_words, W1_scales = pack_weight(np.random.standard_normal((2 * H, INNER)) / np.sqrt(2.0 * H) / s[:, None], FMT)
    b1 = bf(np.random.standard_normal(INNER) * 0.2)
    W2_words, W2_scales = pack_weight(np.random.standard_normal((INNER, VOCAB)) * 0.06, FMT)
    b2 = bf(np.random.standard_normal(VOCAB) * 0.2)
    return {"enc_state": enc_state,
            "dec_state": dec_state,
            "W1_words": W1_words,
            "W1_scales": W1_scales,
            "b1": b1,
            "W2_words": W2_words,
            "W2_scales": W2_scales,
            "b2": b2}


def reference(enc_state, dec_state, W1_words, W1_scales, b1, W2_words, W2_scales, b2):
    W1 = unpack_weight(W1_words, W1_scales, FMT)
    W2 = unpack_weight(W2_words, W2_scales, FMT)
    enc_proj = mxq(f64(enc_state), 2, "e4m3") @ W1[:H]
    dec_proj = mxq(f64(dec_state), 2, "e4m3") @ W1[H:]
    hidden = np.tanh(enc_proj[:, :, None, :] + dec_proj[:, None, :, :] + f64(b1))
    logits = (mxq(hidden, 3, "e4m3") @ W2) + f64(b2)
    return log_softmax(logits)

@@ -1,0 +1,494 @@
+import math
+from contextlib import ExitStack
+
+import concourse.mybir as mybir
+from concourse.masks import make_identity
+
+F32 = mybir.dt.float32
+BF16 = mybir.dt.bfloat16
+I32 = mybir.dt.int32
+U32 = mybir.dt.uint32
+U8 = mybir.dt.uint8
+FP8X4 = mybir.dt.float8_e4m3fn_x4
+ALU = mybir.AluOpType
+ACTF = mybir.ActivationFunctionType
+AX = mybir.AxisListType
+
+P = 128
+NB, NTE, NU, NH = 4, 64, 32, 512
+INNER, VOCAB = 512, 1024
+NT = NB * NTE * NU // P
+TPB = NT // NB
+FLOPS = 2 * NB * NTE * NU * INNER * VOCAB + 2 * NB * (NTE + NU) * NH * INNER
+
+MANUAL = False
+LA, LB, LC, LD, LE, LG = 0, 2, 3, 4, 5, 10
+DVE_TILES = ()
+POOL_TILES = (1, 3, 5, 7, 9, 11, 13, 15, 24, 30, 40, 46, 56)
+POOL_AHEAD = 12
+DVE_AHEAD = 2
+PREP_LEAD = 8
+GROUPS = (8, 8, 8, 8, 8, 8, 8, 4, 2, 2)
+NZ = 24
+
+LN2 = math.log(2.0)
+C0 = 2.0 * math.sqrt(2.0)
+EXPMASK = 0x7F800000
+ATANH_C = (
+    1.0000000000046205,
+    0.33333332564284207,
+    0.20000204355386844,
+    0.14266770007453417,
+    0.11822713435926986,
+)
+
+
+def tile_transducer_kernel(
+    tc, enc_state, dec_state, W1_words, W1_scales, b1, W2_words, W2_scales, b2, out
+):
+    nc = tc.nc
+    out_rows = out.flatten_outer_dims()
+    with ExitStack() as ctx:
+        if MANUAL:
+            ctx.enter_context(tc.manual_schedule())
+        const = ctx.enter_context(tc.tile_pool(name="const", bufs=1))
+        ps_pre = ctx.enter_context(tc.psum_pool(name="ps_pre", bufs=4))
+        ps_lg = ctx.enter_context(tc.psum_pool(name="ps_lg", bufs=4))
+        hid_pool = ctx.enter_context(tc.tile_pool(name="hid", bufs=4))
+        hc_pool = ctx.enter_context(tc.tile_pool(name="hc", bufs=6))
+        add_pool = ctx.enter_context(tc.tile_pool(name="addp", bufs=10))
+        z_pool = ctx.enter_context(tc.tile_pool(name="zp", bufs=NZ))
+        junk_pool = ctx.enter_context(tc.tile_pool(name="junk", bufs=2))
+        stat_pool = ctx.enter_context(tc.tile_pool(name="stat", bufs=8))
+        ch_pool = ctx.enter_context(tc.tile_pool(name="chain", bufs=3))
+
+        warm = const.tile([P, 1], F32, name="warm")
+        nc.vector.memset(warm[:], 0.0)
+        xe = const.tile([P, 2, NH], BF16, name="xe", align_bytes=64)
+        nc.scalar.dma_start(
+            out=xe[:], in_=enc_state.flatten_outer_dims().rearrange("(e p) k -> p e k", p=P)
+        )
+        xd = const.tile([P, NH], BF16, name="xd", align_bytes=64)
+        nc.scalar.dma_start(out=xd[:], in_=dec_state.flatten_outer_dims())
+        warm2 = const.tile([P, 1], F32, name="warm2")
+        nc.scalar.activation(out=warm2[:], in_=warm[:], func=ACTF.Exp)
+
+        w1s = const.tile([P, 2, INNER], U8, name="w1s", align_bytes=64)
+        nc.vector.memset(w1s[:].bitcast(I32), 0)
+        w2s = const.tile([P, VOCAB], U8, name="w2s", align_bytes=64)
+        nc.vector.memset(w2s[:].bitcast(I32), 0)
+        b1st = const.tile([P, INNER], BF16, name="b1st", align_bytes=64)
+        nc.vector.memset(b1st[:].bitcast(I32), 0)
+        gx = const.tile([P, 8, P, 4], BF16, name="gx", align_bytes=64)
+        nc.vector.memset(gx[:].bitcast(I32), 0)
+
+        for q in range(4):
+            nc.sync.dma_start(
+                out=w1s[32 * q : 32 * q + 4, :, :].bitcast(I32),
+                in_=W1_scales[:, 4 * q : 4 * q + 4, :].rearrange("g r n -> r g n").bitcast(I32),
+            )
+        w1w = const.tile([P, 2, INNER], U32, name="w1w", align_bytes=64)
+        nc.sync.dma_start(
+            out=w1w[:].bitcast(I32),
+            in_=W1_words.rearrange("g p n t -> p g (n t)").bitcast(I32),
+        )
+        nc.sync.dma_start(out=b1st[96:97, :], in_=b1.unsqueeze(0))
+        for q in range(4):
+            nc.sync.dma_start(
+                out=w2s[32 * q : 32 * q + 4, :].bitcast(I32),
+                in_=W2_scales[0, 4 * q : 4 * q + 4, :].bitcast(I32),
+            )
+        w2w = const.tile([P, VOCAB], U32, name="w2w", align_bytes=64)
+        nc.sync.dma_start(
+            out=w2w[:].bitcast(I32), in_=W2_words[0].rearrange("p n t -> p (n t)").bitcast(I32)
+        )
+        b2bf = const.tile([P, VOCAB], BF16, name="b2bf")
+        nc.scalar.dma_start(out=b2bf[:], in_=b2.partition_broadcast(P))
+
+        ident = const.tile([P, P], F32, name="ident")
+        make_identity(nc, ident[:])
+        usel = const.tile([P, NU], F32, name="usel")
+        nc.vector.tensor_scalar(
+            out=usel[:], in0=ident[:, 64:96], scalar1=ident[:, 96:97], scalar2=None, op0=ALU.add
+        )
+        sel = const.tile([P, NTE, NU], F32, name="sel")
+        nc.vector.tensor_tensor(
+            out=sel[:],
+            in0=ident[:, 0:NTE].unsqueeze(2).to_broadcast([P, NTE, NU]),
+            in1=usel[:].unsqueeze(1).to_broadcast([P, NTE, NU]),
+            op=ALU.add,
+        )
+        sel2 = sel[:].rearrange("c t u -> c (t u)")
+
+        xew = xe[:].bitcast(F32)
+        xdw = xd[:].bitcast(F32)
+        gxw = gx[:].bitcast(F32)
+        xt0 = ps_pre.tile([P, 2, P], F32, name="xt0", tag="pre")
+        xtd = ps_pre.tile([P, 2, P], F32, name="xtd", tag="pre")
+        xt1 = ps_pre.tile([P, 2, P], F32, name="xt1", tag="pre")
+        for u in range(2):
+            nc.tensor.transpose(out=xt0[:, u, :], in_=xew[:, 0, u:256:2], identity=ident[:])
+        for u in range(2):
+            nc.tensor.transpose(out=xtd[:, u, :], in_=xdw[:, u:256:2], identity=ident[:])
+        for u in range(2):
+            nc.tensor.transpose(out=xt1[:, u, :], in_=xew[:, 1, u:256:2], identity=ident[:])
+        nc.vector.tensor_copy(
+            out=gxw[:, 0:4:2, 0:NTE, :], in_=xt0[:].rearrange("p u (b t) -> p b t u", b=2)
+        )
+        nc.scalar.copy(
+            out=gxw[:, 1:8:2, 64:96, :], in_=xtd[:].rearrange("p u (b v) -> p b v u", b=4)
+        )
+        nc.scalar.copy(
+            out=gxw[:, 4:8:2, 0:NTE, :], in_=xt1[:].rearrange("p u (b t) -> p b t u", b=2)
+        )
+        cx = const.tile([P, 8, P], U32, name="cx", align_bytes=64)
+        sx = const.tile([P, 8, P], U8, name="sx", align_bytes=64)
+
+        def quant_x(s0, ns):
+            nc.vector.quantize_mx(
+                out=cx[:, s0 : s0 + ns, :].rearrange("p s c -> p (s c)").bitcast(FP8X4),
+                scales=sx[:, s0 : s0 + ns, :].rearrange("p s c -> p (s c)"),
+                in_=gx[:, s0 : s0 + ns, :, :].rearrange("p s c t -> p (s c t)"),
+            )
+
+        quant_x(0, 2)
+        quant_x(2, 2)
+        quant_x(4, 4)
+        b2f = const.tile([P, VOCAB], F32, name="b2f")
+        nc.scalar.copy(out=b2f[:], in_=b2bf[:])
+
+        pj = [const.tile([P, 4, P], F32, name="pj%d" % b) for b in range(NB)]
+        for b in range(NB):
+            nc.vector.tensor_copy(
+                out=pj[b][96:128, :, :], in_=b1st[96:128, :].rearrange("c (p j) -> c j p", j=4)
+            )
+        ptab = {}
+        dtab = {}
+        hold = {}
+        other = set(DVE_TILES) | set(POOL_TILES)
+        need_pt = set(i // TPB for i in other)
+
+        def prep0(b):
+            pp = ps_pre.tile([P, INNER], F32, name="pp%d" % b, tag="pre")
+            hold[b] = pp
+            for g in range(2):
+                nc.tensor.matmul_mx(
+                    out=pp[:],
+                    lhsT=cx[:, 2 * b + g, :].bitcast(FP8X4),
+                    lhsT_scale=sx[:, 2 * b + g, :],
+                    rhs=w1w[:, g, :].bitcast(FP8X4),
+                    rhs_scale=w1s[:, g, :],
+                    start=(g == 0),
+                    stop=(g == 1),
+                )
+
+        def prep1(b):
+            nc.scalar.copy(
+                out=pj[b][0:96, :, :], in_=hold[b][0:96, :].rearrange("c (p j) -> c j p", j=4)
+            )
+
+        def prep2(b):
+            if b not in need_pt:
+                return
+            pt = ps_pre.tile([P, 4, P], F32, name="pt%d" % b, tag="pre")
+            hold[b] = pt
+            for j in range(4):
+                nc.tensor.transpose(out=pt[:, j, :], in_=pj[b][:, j, :], identity=ident[:])
+
+        def prep3(b):
+            if b not in need_pt:
+                return
+            ptab[b] = const.tile([P, P, 4], F32, name="ptab%d" % b)
+            nc.scalar.copy(out=ptab[b][:], in_=hold[b][:].rearrange("p j c -> p c j"))
+            dtab[b] = const.tile([P, NU, 4], F32, name="dtab%d" % b)
+            nc.gpsimd.tensor_tensor(
+                out=dtab[b][:],
+                in0=ptab[b][:, 64:96, :],
+                in1=ptab[b][:, 96:97, :].to_broadcast([P, NU, 4]),
+                op=ALU.add,
+            )
+
+        preps = (prep0, prep1, prep2, prep3)
+        for f in preps:
+            f(0)
+
+        g_of = []
+        g_lo = []
+        for k, n_k in enumerate(GROUPS):
+            g_lo.append(len(g_of))
+            g_of.extend([k] * n_k)
+        assert len(g_of) == NT
+        f_end = {}
+        for k, n_k in enumerate(GROUPS):
+            a = g_lo[k]
+            cuts = [1, 1] if k == 0 else []
+            while sum(cuts) < n_k:
+                cuts.append(min(2, n_k - sum(cuts)))
+            pos = a
+            for c in cuts:
+                f_end[pos + c - 1] = (pos - a, c)
+                pos += c
+
+        pre_of = {}
+        hid_of = {}
+        hc_of = {}
+        lg_of = {}
+        z_of = {}
+        stat = {}
+        chains = []
+        state = {"late": False, "tog": 0}
+
+        def get_stat(k):
+            if k not in stat:
+                stat[k] = (
+                    None,
+                    stat_pool.tile([P, 8], F32, name="negm%d" % k, tag="negm"),
+                    stat_pool.tile([P, 8], F32, name="ssum%d" % k, tag="ssum"),
+                    stat_pool.tile([P, 8], F32, name="negc%d" % k, tag="negc"),
+                )
+            return stat[k]
+
+        def add_tile(eng, i):
+            b, ti = i // TPB, i % TPB
+            pre = add_pool.tile([P, 4, NU, 4], F32, name="apre%d" % i, tag="apre")
+            pre_of[i] = pre
+            eng.tensor_tensor(
+                out=pre[:],
+                in0=ptab[b][:, 4 * ti : 4 * ti + 4, :].unsqueeze(2).to_broadcast([P, 4, NU, 4]),
+                in1=dtab[b][:].unsqueeze(1).to_broadcast([P, 4, NU, 4]),
+                op=ALU.add,
+            )
+
+        def st_a(i):
+            b, ti = i // TPB, i % TPB
+            pre = ps_pre.tile([P, 4, P], F32, name="pre%d" % i, tag="pre")
+            pre_of[i] = pre
+            for j in range(4):
+                nc.tensor.matmul(
+                    out=pre[:, j, :],
+                    lhsT=pj[b][:, j, :],
+                    rhs=sel2[:, P * ti : P * ti + P],
+                    start=True,
+                    stop=True,
+                )
+
+        def st_b(i):
+            hid = hid_pool.tile([P, P, 4], BF16, name="hid%d" % i, tag="hid", align_bytes=64)
+            hid_of[i] = hid
+            if i in other:
+                nc.scalar.activation(
+                    out=hid[:].rearrange("p r j -> p (r j)"),
+                    in_=pre_of[i][:].rearrange("p a u j -> p (a u j)"),
+                    func=ACTF.Tanh,
+                )
+            else:
+                nc.scalar.activation(
+                    out=hid[:], in_=pre_of[i][:].rearrange("p j r -> p r j"), func=ACTF.Tanh
+                )
+
+        def st_c(i):
+            hc = hc_pool.tile([P, P], U32, name="hc%d" % i, tag="hc", align_bytes=64)
+            hs = hc_pool.tile([P, P], U8, name="hs%d" % i, tag="hs", align_bytes=64)
+            hc_of[i] = (hc, hs)
+            nc.vector.quantize_mx(
+                out=hc[:].bitcast(FP8X4),
+                scales=hs[:],
+                in_=hid_of[i][:].rearrange("p r j -> p (r j)"),
+            )
+
+        def st_d(i):
+            hc, hs = hc_of[i]
+            lg_of[i] = []
+            for h in range(2):
+                lg = ps_lg.tile([P, 512], F32, name="lg%d_%d" % (i, h), tag="lg")
+                lg_of[i].append(lg)
+                nc.tensor.matmul_mx(
+                    out=lg[:],
+                    lhsT=hc[:].bitcast(FP8X4),
+                    lhsT_scale=hs[:],
+                    rhs=w2w[:, 512 * h : 512 * h + 512].bitcast(FP8X4),
+                    rhs_scale=w2s[:, 512 * h : 512 * h + 512],
+                    start=True,
+                    stop=True,
+                )
+
+        def st_e(i, h):
+            k = g_of[i]
+            c = i - g_lo[k]
+            mn = get_stat(k)[0]
+            if h == 0:
+                z_of[i] = z_pool.tile([P, VOCAB], F32, name="z%d" % i, tag="z")
+            nc.vector.tensor_tensor(
+                out=z_of[i][:, 512 * h : 512 * h + 512],
+                in0=lg_of[i][h][:],
+                in1=b2f[:, 512 * h : 512 * h + 512],
+                op=ALU.add,
+            )
+
+        def st_f(i):
+            k = g_of[i]
+            c = i - g_lo[k]
+            negm = get_stat(k)[1]
+            nc.vector.tensor_reduce(
+                out=negm[:, c : c + 1], in_=z_of[i][:], axis=AX.X, op=ALU.max, negate=True
+            )
+
+        def st_g(i):
+            k = g_of[i]
+            c = i - g_lo[k]
+            negm, ssum = get_stat(k)[1], get_stat(k)[2]
+            junk = junk_pool.tile([P, VOCAB], BF16, name="junk%d" % i, tag="junk")
+            nc.scalar.activation(
+                out=junk[:],
+                in_=z_of[i][:],
+                func=ACTF.Exp,
+                bias=negm[:, c : c + 1],
+                scale=1.0,
+                accum_out=ssum[:, c : c + 1],
+            )
+
+        def final_part(eng_name, i, lo, hi):
+            k = g_of[i]
+            c = i - g_lo[k]
+            negc = get_stat(k)[3]
+            zz = z_of[i][:, lo:hi]
+            if eng_name == "act":
+                nc.scalar.activation(
+                    out=zz, in_=zz, func=ACTF.Identity, bias=negc[:, c : c + 1], scale=1.0
+                )
+            else:
+                eng = nc.vector if eng_name == "dve" else nc.gpsimd
+                eng.tensor_scalar(
+                    out=zz,
+                    in0=zz,
+                    scalar1=1.0,
+                    scalar2=negc[:, c : c + 1],
+                    op0=ALU.mult,
+                    op1=ALU.add,
+                )
+
+        def finals(k):
+            is_ln = k == len(GROUPS) - 1
+            for i in range(g_lo[k], g_lo[k] + GROUPS[k]):
+                if is_ln:
+                    final_part("dve", i, 0, 512)
+                    final_part("act", i, 512, 768)
+                    final_part("pool", i, 768, 1024)
+                elif state["late"]:
+                    final_part("dve", i, 0, 640)
+                    final_part("pool", i, 640, 1024)
+                else:
+                    final_part("pool", i, 0, 1024)
+                nc.sync.dma_start(out=out_rows[P * i : P * i + P, :], in_=z_of[i][:])
+
+        def make_chain(k):
+            n_k = GROUPS[k]
+            mn, negm_t, ssum_t, negc_t = get_stat(k)
+            negm, ssum, negc = negm_t[:, 0:n_k], ssum_t[:, 0:n_k], negc_t[:, 0:n_k]
+            if True:
+                lns = ch_pool.tile([P, 8], F32, name="lns%d" % k, tag="lns")
+                return [
+                    lambda: nc.scalar.activation(out=lns[:, 0:n_k], in_=ssum, func=ACTF.Ln),
+                    lambda: nc.vector.tensor_tensor(
+                        out=negc, in0=negm, in1=lns[:, 0:n_k], op=ALU.subtract
+                    ),
+                ]
+            p2t = ch_pool.tile([P, 8], I32, name="p2_%d" % k, tag="p2")
+            a1t = ch_pool.tile([P, 8], F32, name="a1_%d" % k, tag="a1")
+            mmt = ch_pool.tile([P, 8], F32, name="mm_%d" % k, tag="mm")
+            dnt = ch_pool.tile([P, 8], F32, name="dn_%d" % k, tag="dn")
+            yt = ch_pool.tile([P, 8], F32, name="y_%d" % k, tag="y")
+            y2t = ch_pool.tile([P, 8], F32, name="y2_%d" % k, tag="y2")
+            ut = ch_pool.tile([P, 8], F32, name="u_%d" % k, tag="u")
+            p2, a1, mm, dn = p2t[:, 0:n_k], a1t[:, 0:n_k], mmt[:, 0:n_k], dnt[:, 0:n_k]
+            y, y2, uu = yt[:, 0:n_k], y2t[:, 0:n_k], ut[:, 0:n_k]
+            v = nc.vector
+
+            def horner(coef, other_in):
+                return lambda: v.scalar_tensor_tensor(
+                    out=uu, in0=uu, scalar=coef, in1=other_in, op0=ALU.add, op1=ALU.mult
+                )
+
+            return [
+                lambda: v.tensor_scalar(
+                    out=p2,
+                    in0=ssum.bitcast(I32),
+                    scalar1=EXPMASK,
+                    scalar2=EXPMASK,
+                    op0=ALU.bitwise_xor,
+                    op1=ALU.bitwise_and,
+                ),
+                lambda: v.tensor_tensor(out=mm, in0=ssum, in1=p2.bitcast(F32), op=ALU.mult),
+                lambda: v.tensor_scalar(
+                    out=a1, in0=p2, scalar1=2.0**-23, scalar2=-128.5, op0=ALU.mult, op1=ALU.add
+                ),
+                lambda: v.tensor_scalar(out=dn, in0=mm, scalar1=C0, scalar2=None, op0=ALU.add),
+                lambda: v.scalar_tensor_tensor(
+                    out=a1, in0=a1, scalar=LN2, in1=negm, op0=ALU.mult, op1=ALU.add
+                ),
+                lambda: v.reciprocal(out=dn, in_=dn),
+                lambda: v.scalar_tensor_tensor(
+                    out=y, in0=mm, scalar=C0, in1=dn, op0=ALU.subtract, op1=ALU.mult
+                ),
+                lambda: v.tensor_tensor(out=y2, in0=y, in1=y, op=ALU.mult),
+                lambda: v.tensor_scalar(
+                    out=uu, in0=y2, scalar1=ATANH_C[4], scalar2=None, op0=ALU.mult
+                ),
+                horner(ATANH_C[3], y2),
+                horner(ATANH_C[2], y2),
+                horner(ATANH_C[1], y2),
+                horner(ATANH_C[0], y),
+                lambda: v.scalar_tensor_tensor(
+                    out=negc, in0=uu, scalar=-2.0, in1=a1, op0=ALU.mult, op1=ALU.add
+                ),
+            ]
+
+        def pop_chain(count):
+            for q in range(count):
+                if not chains:
+                    return
+                idx = 1 if (len(chains) > 1 and state["tog"] % 2 == 1) else 0
+                state["tog"] += 1
+                ch = chains[idx]
+                ch[1].pop(0)()
+                if not ch[1]:
+                    chains.pop(idx)
+                    finals(ch[0])
+
+        for n in range(NT + LG + 1):
+            for b in range(1, NB):
+                s = n - (TPB * b - PREP_LEAD)
+                if 0 <= s < 4:
+                    preps[s](b)
+            for i in POOL_TILES:
+                if n == max(0, i + LA - POOL_AHEAD):
+                    add_tile(nc.gpsimd, i)
+            for i in DVE_TILES:
+                if n == max(0, i + LA - DVE_AHEAD):
+                    add_tile(nc.vector, i)
+            if 0 <= n - LC < NT:
+                st_c(n - LC)
+                pop_chain(1)
+            if 0 <= n - LA < NT and (n - LA) not in other:
+                st_a(n - LA)
+            if 0 <= n - LD < NT:
+                st_d(n - LD)
+            if 0 <= n - LG < NT:
+                st_g(n - LG)
+            if 0 <= n - LB < NT:
+                st_b(n - LB)
+            i = n - LG
+            if 0 <= i < NT and (i == NT - 1 or g_of[i + 1] != g_of[i]):
+                chains.append((g_of[i], make_chain(g_of[i])))
+            i = n - LE
+            if 0 <= i < NT:
+                st_e(i, 0)
+                pop_chain(1)
+                st_e(i, 1)
+                pop_chain(1)
+                st_f(i)
+                if i == NT - 1:
+                    state["late"] = True
+            elif i >= NT:
+                pop_chain(8)
+        pop_chain(1000)

@@ -1,4 +1,3 @@
-import math
 from contextlib import ExitStack
 
 import concourse.mybir as mybir
@@ -21,26 +20,21 @@ NT = NB * NTE * NU // P
 TPB = NT // NB
 FLOPS = 2 * NB * NTE * NU * INNER * VOCAB + 2 * NB * (NTE + NU) * NH * INNER
 
-MANUAL = False
-LA, LB, LC, LD, LE, LG = 0, 2, 3, 4, 5, 10
-DVE_TILES = ()
-POOL_TILES = (1, 3, 5, 7, 9, 11, 13, 15, 24, 30, 40, 46, 56)
-POOL_AHEAD = 12
-DVE_AHEAD = 2
-PREP_LEAD = 8
-GROUPS = (8, 8, 8, 8, 8, 8, 8, 4, 2, 2)
+MANUAL = True
+RUN_AHEAD = 8
+POOL_TILES = tuple(range(3, 16))
+QUANT_GROUPS = (1, 1, 2, 2, 2) + (4,) * 14
+LN_GROUPS = (8, 8, 8, 8, 8, 6, 5, 4, 3, 3, 3)
 NZ = 24
 
-LN2 = math.log(2.0)
-C0 = 2.0 * math.sqrt(2.0)
-EXPMASK = 0x7F800000
-ATANH_C = (
-    1.0000000000046205,
-    0.33333332564284207,
-    0.20000204355386844,
-    0.14266770007453417,
-    0.11822713435926986,
-)
+
+def spans(sizes):
+    of, lo = [], []
+    for k, n_k in enumerate(sizes):
+        lo.append(len(of))
+        of.extend([k] * n_k)
+    assert len(of) == NT
+    return of, lo
 
 
 def tile_transducer_kernel(
@@ -55,12 +49,11 @@ def tile_transducer_kernel(
         ps_pre = ctx.enter_context(tc.psum_pool(name="ps_pre", bufs=4))
         ps_lg = ctx.enter_context(tc.psum_pool(name="ps_lg", bufs=4))
         hid_pool = ctx.enter_context(tc.tile_pool(name="hid", bufs=4))
-        hc_pool = ctx.enter_context(tc.tile_pool(name="hc", bufs=6))
-        add_pool = ctx.enter_context(tc.tile_pool(name="addp", bufs=10))
+        hc_pool = ctx.enter_context(tc.tile_pool(name="hc", bufs=4))
+        add_pool = ctx.enter_context(tc.tile_pool(name="addp", bufs=8))
         z_pool = ctx.enter_context(tc.tile_pool(name="zp", bufs=NZ))
         junk_pool = ctx.enter_context(tc.tile_pool(name="junk", bufs=2))
         stat_pool = ctx.enter_context(tc.tile_pool(name="stat", bufs=8))
-        ch_pool = ctx.enter_context(tc.tile_pool(name="chain", bufs=3))
 
         warm = const.tile([P, 1], F32, name="warm")
         nc.vector.memset(warm[:], 0.0)
@@ -102,8 +95,8 @@ def tile_transducer_kernel(
         nc.sync.dma_start(
             out=w2w[:].bitcast(I32), in_=W2_words[0].rearrange("p n t -> p (n t)").bitcast(I32)
         )
-        b2bf = const.tile([P, VOCAB], BF16, name="b2bf")
-        nc.scalar.dma_start(out=b2bf[:], in_=b2.partition_broadcast(P))
+        b2bc = const.tile([P, VOCAB], BF16, name="b2bc")
+        nc.scalar.dma_start(out=b2bc[:], in_=b2.partition_broadcast(P))
 
         ident = const.tile([P, P], F32, name="ident")
         make_identity(nc, ident[:])
@@ -151,24 +144,23 @@ def tile_transducer_kernel(
                 in_=gx[:, s0 : s0 + ns, :, :].rearrange("p s c t -> p (s c t)"),
             )
 
-        quant_x(0, 2)
-        quant_x(2, 2)
-        quant_x(4, 4)
-        b2f = const.tile([P, VOCAB], F32, name="b2f")
-        nc.scalar.copy(out=b2f[:], in_=b2bf[:])
-
         pj = [const.tile([P, 4, P], F32, name="pj%d" % b) for b in range(NB)]
-        for b in range(NB):
+
+        def bias_rows(b):
             nc.vector.tensor_copy(
                 out=pj[b][96:128, :, :], in_=b1st[96:128, :].rearrange("c (p j) -> c j p", j=4)
             )
-        ptab = {}
-        dtab = {}
-        hold = {}
-        other = set(DVE_TILES) | set(POOL_TILES)
-        need_pt = set(i // TPB for i in other)
 
-        def prep0(b):
+        quant_x(0, 2)
+        bias_rows(0)
+        quant_x(2, 2)
+        quant_x(4, 4)
+        for b in range(1, NB):
+            bias_rows(b)
+
+        hold = {}
+
+        def project(b):
             pp = ps_pre.tile([P, INNER], F32, name="pp%d" % b, tag="pre")
             hold[b] = pp
             for g in range(2):
@@ -182,80 +174,53 @@ def tile_transducer_kernel(
                     stop=(g == 1),
                 )
 
-        def prep1(b):
+        def project_out(b):
             nc.scalar.copy(
                 out=pj[b][0:96, :, :], in_=hold[b][0:96, :].rearrange("c (p j) -> c j p", j=4)
             )
 
-        def prep2(b):
-            if b not in need_pt:
-                return
-            pt = ps_pre.tile([P, 4, P], F32, name="pt%d" % b, tag="pre")
-            hold[b] = pt
-            for j in range(4):
-                nc.tensor.transpose(out=pt[:, j, :], in_=pj[b][:, j, :], identity=ident[:])
+        project(0)
+        project_out(0)
 
-        def prep3(b):
-            if b not in need_pt:
-                return
-            ptab[b] = const.tile([P, P, 4], F32, name="ptab%d" % b)
-            nc.scalar.copy(out=ptab[b][:], in_=hold[b][:].rearrange("p j c -> p c j"))
-            dtab[b] = const.tile([P, NU, 4], F32, name="dtab%d" % b)
+        ptab = const.tile([P, P, 4], F32, name="ptab")
+        dtab = const.tile([P, NU, 4], F32, name="dtab")
+
+        def tables_pe():
+            pt = ps_pre.tile([P, 4, P], F32, name="pt", tag="pre")
+            hold["pt"] = pt
+            for j in range(4):
+                nc.tensor.transpose(out=pt[:, j, :], in_=pj[0][:, j, :], identity=ident[:])
+
+        def tables_out():
+            nc.scalar.copy(out=ptab[:], in_=hold["pt"][:].rearrange("p j c -> p c j"))
             nc.gpsimd.tensor_tensor(
-                out=dtab[b][:],
-                in0=ptab[b][:, 64:96, :],
-                in1=ptab[b][:, 96:97, :].to_broadcast([P, NU, 4]),
+                out=dtab[:],
+                in0=ptab[:, 64:96, :],
+                in1=ptab[:, 96:97, :].to_broadcast([P, NU, 4]),
                 op=ALU.add,
             )
 
-        preps = (prep0, prep1, prep2, prep3)
-        for f in preps:
-            f(0)
-
-        g_of = []
-        g_lo = []
-        for k, n_k in enumerate(GROUPS):
-            g_lo.append(len(g_of))
-            g_of.extend([k] * n_k)
-        assert len(g_of) == NT
-        f_end = {}
-        for k, n_k in enumerate(GROUPS):
-            a = g_lo[k]
-            cuts = [1, 1] if k == 0 else []
-            while sum(cuts) < n_k:
-                cuts.append(min(2, n_k - sum(cuts)))
-            pos = a
-            for c in cuts:
-                f_end[pos + c - 1] = (pos - a, c)
-                pos += c
-
-        pre_of = {}
-        hid_of = {}
-        hc_of = {}
-        lg_of = {}
-        z_of = {}
-        stat = {}
-        chains = []
-        state = {"late": False, "tog": 0}
+        q_of, q_lo = spans(QUANT_GROUPS)
+        g_of, g_lo = spans(LN_GROUPS)
+        pre_of, hid_of, hc_of, lg_of, z_of, stat = {}, {}, {}, {}, {}, {}
 
         def get_stat(k):
             if k not in stat:
                 stat[k] = (
-                    None,
                     stat_pool.tile([P, 8], F32, name="negm%d" % k, tag="negm"),
                     stat_pool.tile([P, 8], F32, name="ssum%d" % k, tag="ssum"),
+                    stat_pool.tile([P, 8], F32, name="lns%d" % k, tag="lns"),
                     stat_pool.tile([P, 8], F32, name="negc%d" % k, tag="negc"),
                 )
             return stat[k]
 
-        def add_tile(eng, i):
-            b, ti = i // TPB, i % TPB
+        def st_add(i):
             pre = add_pool.tile([P, 4, NU, 4], F32, name="apre%d" % i, tag="apre")
             pre_of[i] = pre
-            eng.tensor_tensor(
+            nc.gpsimd.tensor_tensor(
                 out=pre[:],
-                in0=ptab[b][:, 4 * ti : 4 * ti + 4, :].unsqueeze(2).to_broadcast([P, 4, NU, 4]),
-                in1=dtab[b][:].unsqueeze(1).to_broadcast([P, 4, NU, 4]),
+                in0=ptab[:, 4 * i : 4 * i + 4, :].unsqueeze(2).to_broadcast([P, 4, NU, 4]),
+                in1=dtab[:].unsqueeze(1).to_broadcast([P, 4, NU, 4]),
                 op=ALU.add,
             )
 
@@ -273,39 +238,47 @@ def tile_transducer_kernel(
                 )
 
         def st_b(i):
-            hid = hid_pool.tile([P, P, 4], BF16, name="hid%d" % i, tag="hid", align_bytes=64)
-            hid_of[i] = hid
-            if i in other:
+            q = q_of[i]
+            pos = i - q_lo[q]
+            if pos == 0:
+                hid_of[q] = hid_pool.tile(
+                    [P, QUANT_GROUPS[q] * P, 4], BF16, name="hid%d" % q, tag="hid", align_bytes=64
+                )
+            dst = hid_of[q][:, P * pos : P * pos + P, :]
+            if i in POOL_TILES:
                 nc.scalar.activation(
-                    out=hid[:].rearrange("p r j -> p (r j)"),
+                    out=dst.rearrange("p r j -> p (r j)"),
                     in_=pre_of[i][:].rearrange("p a u j -> p (a u j)"),
                     func=ACTF.Tanh,
                 )
             else:
                 nc.scalar.activation(
-                    out=hid[:], in_=pre_of[i][:].rearrange("p j r -> p r j"), func=ACTF.Tanh
+                    out=dst, in_=pre_of[i][:].rearrange("p j r -> p r j"), func=ACTF.Tanh
                 )
 
-        def st_c(i):
-            hc = hc_pool.tile([P, P], U32, name="hc%d" % i, tag="hc", align_bytes=64)
-            hs = hc_pool.tile([P, P], U8, name="hs%d" % i, tag="hs", align_bytes=64)
-            hc_of[i] = (hc, hs)
+        def st_c(q):
+            n_q = QUANT_GROUPS[q]
+            hc = hc_pool.tile([P, n_q * P], U32, name="hc%d" % q, tag="hc", align_bytes=64)
+            hs = hc_pool.tile([P, n_q * P], U8, name="hs%d" % q, tag="hs", align_bytes=64)
+            hc_of[q] = (hc, hs)
             nc.vector.quantize_mx(
                 out=hc[:].bitcast(FP8X4),
                 scales=hs[:],
-                in_=hid_of[i][:].rearrange("p r j -> p (r j)"),
+                in_=hid_of[q][:].rearrange("p r j -> p (r j)"),
             )
 
         def st_d(i):
-            hc, hs = hc_of[i]
+            q = q_of[i]
+            pos = i - q_lo[q]
+            hc, hs = hc_of[q]
             lg_of[i] = []
             for h in range(2):
                 lg = ps_lg.tile([P, 512], F32, name="lg%d_%d" % (i, h), tag="lg")
                 lg_of[i].append(lg)
                 nc.tensor.matmul_mx(
                     out=lg[:],
-                    lhsT=hc[:].bitcast(FP8X4),
-                    lhsT_scale=hs[:],
+                    lhsT=hc[:, P * pos : P * pos + P].bitcast(FP8X4),
+                    lhsT_scale=hs[:, P * pos : P * pos + P],
                     rhs=w2w[:, 512 * h : 512 * h + 512].bitcast(FP8X4),
                     rhs_scale=w2s[:, 512 * h : 512 * h + 512],
                     start=True,
@@ -313,30 +286,28 @@ def tile_transducer_kernel(
                 )
 
         def st_e(i, h):
-            k = g_of[i]
-            c = i - g_lo[k]
-            mn = get_stat(k)[0]
             if h == 0:
                 z_of[i] = z_pool.tile([P, VOCAB], F32, name="z%d" % i, tag="z")
             nc.vector.tensor_tensor(
                 out=z_of[i][:, 512 * h : 512 * h + 512],
                 in0=lg_of[i][h][:],
-                in1=b2f[:, 512 * h : 512 * h + 512],
+                in1=b2bc[:, 512 * h : 512 * h + 512],
                 op=ALU.add,
             )
 
-        def st_f(i):
-            k = g_of[i]
-            c = i - g_lo[k]
-            negm = get_stat(k)[1]
+        def st_m(i):
+            c = i - g_lo[g_of[i]]
             nc.vector.tensor_reduce(
-                out=negm[:, c : c + 1], in_=z_of[i][:], axis=AX.X, op=ALU.max, negate=True
+                out=get_stat(g_of[i])[0][:, c : c + 1],
+                in_=z_of[i][:],
+                axis=AX.X,
+                op=ALU.max,
+                negate=True,
             )
 
         def st_g(i):
-            k = g_of[i]
-            c = i - g_lo[k]
-            negm, ssum = get_stat(k)[1], get_stat(k)[2]
+            c = i - g_lo[g_of[i]]
+            negm, ssum = get_stat(g_of[i])[0], get_stat(g_of[i])[1]
             junk = junk_pool.tile([P, VOCAB], BF16, name="junk%d" % i, tag="junk")
             nc.scalar.activation(
                 out=junk[:],
@@ -347,10 +318,22 @@ def tile_transducer_kernel(
                 accum_out=ssum[:, c : c + 1],
             )
 
+        def st_ln(k):
+            n_k = LN_GROUPS[k]
+            nc.scalar.activation(
+                out=get_stat(k)[2][:, 0:n_k], in_=get_stat(k)[1][:, 0:n_k], func=ACTF.Ln
+            )
+
+        def st_negc(k):
+            n_k = LN_GROUPS[k]
+            negm, ssum, lns, negc = get_stat(k)
+            nc.vector.tensor_tensor(
+                out=negc[:, 0:n_k], in0=negm[:, 0:n_k], in1=lns[:, 0:n_k], op=ALU.subtract
+            )
+
         def final_part(eng_name, i, lo, hi):
-            k = g_of[i]
-            c = i - g_lo[k]
-            negc = get_stat(k)[3]
+            c = i - g_lo[g_of[i]]
+            negc = get_stat(g_of[i])[3]
             zz = z_of[i][:, lo:hi]
             if eng_name == "act":
                 nc.scalar.activation(
@@ -367,128 +350,66 @@ def tile_transducer_kernel(
                     op1=ALU.add,
                 )
 
-        def finals(k):
-            is_ln = k == len(GROUPS) - 1
-            for i in range(g_lo[k], g_lo[k] + GROUPS[k]):
-                if is_ln:
+        def finals(k, late):
+            for i in range(g_lo[k], g_lo[k] + LN_GROUPS[k]):
+                if k == len(LN_GROUPS) - 1:
                     final_part("dve", i, 0, 512)
                     final_part("act", i, 512, 768)
                     final_part("pool", i, 768, 1024)
-                elif state["late"]:
+                elif late:
                     final_part("dve", i, 0, 640)
                     final_part("pool", i, 640, 1024)
                 else:
                     final_part("pool", i, 0, 1024)
                 nc.sync.dma_start(out=out_rows[P * i : P * i + P, :], in_=z_of[i][:])
 
-        def make_chain(k):
-            n_k = GROUPS[k]
-            mn, negm_t, ssum_t, negc_t = get_stat(k)
-            negm, ssum, negc = negm_t[:, 0:n_k], ssum_t[:, 0:n_k], negc_t[:, 0:n_k]
-            if True:
-                lns = ch_pool.tile([P, 8], F32, name="lns%d" % k, tag="lns")
-                return [
-                    lambda: nc.scalar.activation(out=lns[:, 0:n_k], in_=ssum, func=ACTF.Ln),
-                    lambda: nc.vector.tensor_tensor(
-                        out=negc, in0=negm, in1=lns[:, 0:n_k], op=ALU.subtract
-                    ),
-                ]
-            p2t = ch_pool.tile([P, 8], I32, name="p2_%d" % k, tag="p2")
-            a1t = ch_pool.tile([P, 8], F32, name="a1_%d" % k, tag="a1")
-            mmt = ch_pool.tile([P, 8], F32, name="mm_%d" % k, tag="mm")
-            dnt = ch_pool.tile([P, 8], F32, name="dn_%d" % k, tag="dn")
-            yt = ch_pool.tile([P, 8], F32, name="y_%d" % k, tag="y")
-            y2t = ch_pool.tile([P, 8], F32, name="y2_%d" % k, tag="y2")
-            ut = ch_pool.tile([P, 8], F32, name="u_%d" % k, tag="u")
-            p2, a1, mm, dn = p2t[:, 0:n_k], a1t[:, 0:n_k], mmt[:, 0:n_k], dnt[:, 0:n_k]
-            y, y2, uu = yt[:, 0:n_k], y2t[:, 0:n_k], ut[:, 0:n_k]
-            v = nc.vector
+        def front(i):
+            return min(NT - 1, i + min(RUN_AHEAD, 1 + i))
 
-            def horner(coef, other_in):
-                return lambda: v.scalar_tensor_tensor(
-                    out=uu, in0=uu, scalar=coef, in1=other_in, op0=ALU.add, op1=ALU.mult
-                )
-
-            return [
-                lambda: v.tensor_scalar(
-                    out=p2,
-                    in0=ssum.bitcast(I32),
-                    scalar1=EXPMASK,
-                    scalar2=EXPMASK,
-                    op0=ALU.bitwise_xor,
-                    op1=ALU.bitwise_and,
-                ),
-                lambda: v.tensor_tensor(out=mm, in0=ssum, in1=p2.bitcast(F32), op=ALU.mult),
-                lambda: v.tensor_scalar(
-                    out=a1, in0=p2, scalar1=2.0**-23, scalar2=-128.5, op0=ALU.mult, op1=ALU.add
-                ),
-                lambda: v.tensor_scalar(out=dn, in0=mm, scalar1=C0, scalar2=None, op0=ALU.add),
-                lambda: v.scalar_tensor_tensor(
-                    out=a1, in0=a1, scalar=LN2, in1=negm, op0=ALU.mult, op1=ALU.add
-                ),
-                lambda: v.reciprocal(out=dn, in_=dn),
-                lambda: v.scalar_tensor_tensor(
-                    out=y, in0=mm, scalar=C0, in1=dn, op0=ALU.subtract, op1=ALU.mult
-                ),
-                lambda: v.tensor_tensor(out=y2, in0=y, in1=y, op=ALU.mult),
-                lambda: v.tensor_scalar(
-                    out=uu, in0=y2, scalar1=ATANH_C[4], scalar2=None, op0=ALU.mult
-                ),
-                horner(ATANH_C[3], y2),
-                horner(ATANH_C[2], y2),
-                horner(ATANH_C[1], y2),
-                horner(ATANH_C[0], y),
-                lambda: v.scalar_tensor_tensor(
-                    out=negc, in0=uu, scalar=-2.0, in1=a1, op0=ALU.mult, op1=ALU.add
-                ),
-            ]
-
-        def pop_chain(count):
-            for q in range(count):
-                if not chains:
-                    return
-                idx = 1 if (len(chains) > 1 and state["tog"] % 2 == 1) else 0
-                state["tog"] += 1
-                ch = chains[idx]
-                ch[1].pop(0)()
-                if not ch[1]:
-                    chains.pop(idx)
-                    finals(ch[0])
-
-        for n in range(NT + LG + 1):
+        nxt = {"a": 0, "b": 0, "add": 0, "q": 0}
+        q_step = {}
+        waiting = []
+        for i in range(NT + 4):
             for b in range(1, NB):
-                s = n - (TPB * b - PREP_LEAD)
-                if 0 <= s < 4:
-                    preps[s](b)
-            for i in POOL_TILES:
-                if n == max(0, i + LA - POOL_AHEAD):
-                    add_tile(nc.gpsimd, i)
-            for i in DVE_TILES:
-                if n == max(0, i + LA - DVE_AHEAD):
-                    add_tile(nc.vector, i)
-            if 0 <= n - LC < NT:
-                st_c(n - LC)
-                pop_chain(1)
-            if 0 <= n - LA < NT and (n - LA) not in other:
-                st_a(n - LA)
-            if 0 <= n - LD < NT:
-                st_d(n - LD)
-            if 0 <= n - LG < NT:
-                st_g(n - LG)
-            if 0 <= n - LB < NT:
-                st_b(n - LB)
-            i = n - LG
-            if 0 <= i < NT and (i == NT - 1 or g_of[i + 1] != g_of[i]):
-                chains.append((g_of[i], make_chain(g_of[i])))
-            i = n - LE
-            if 0 <= i < NT:
+                if i == TPB * b - RUN_AHEAD - 6:
+                    project(b)
+                if i == TPB * b - RUN_AHEAD - 5:
+                    project_out(b)
+            while nxt["a"] <= min(NT - 1, front(i) + (0 if i == 0 else 1)):
+                if nxt["a"] not in POOL_TILES:
+                    st_a(nxt["a"])
+                if nxt["a"] == 0:
+                    tables_pe()
+                nxt["a"] += 1
+            while nxt["b"] <= front(i) and nxt["b"] < NT:
+                t = nxt["b"]
+                while nxt["add"] < len(POOL_TILES) and POOL_TILES[nxt["add"]] <= front(i) + 3 and t > 0:
+                    st_add(POOL_TILES[nxt["add"]])
+                    nxt["add"] += 1
+                st_b(t)
+                if t == 0:
+                    tables_out()
+                if t + 1 == NT or q_of[t + 1] != q_of[t]:
+                    q_step[q_of[t]] = i
+                nxt["b"] += 1
+            while nxt["q"] in q_step and (q_step[nxt["q"]] < i or q_lo[nxt["q"]] <= i):
+                st_c(nxt["q"])
+                nxt["q"] += 1
+            if i < NT:
+                st_d(i)
                 st_e(i, 0)
-                pop_chain(1)
+            if 1 <= i <= NT:
+                st_m(i - 1)
+            if i < NT:
                 st_e(i, 1)
-                pop_chain(1)
-                st_f(i)
-                if i == NT - 1:
-                    state["late"] = True
-            elif i >= NT:
-                pop_chain(8)
-        pop_chain(1000)
+            while waiting and (waiting[0][1] <= i or i >= NT):
+                k = waiting.pop(0)[0]
+                st_negc(k)
+                finals(k, i >= NT)
+            t = i - 2
+            if 0 <= t < NT:
+                st_g(t)
+                if t + 1 == NT or g_of[t + 1] != g_of[t]:
+                    st_ln(g_of[t])
+                    waiting.append((g_of[t], i + 1))
+        assert not waiting

@@ -24,8 +24,8 @@ MANUAL = True
 RUN_AHEAD = 8
 POOL_TILES = tuple(range(3, 16))
 QUANT_GROUPS = (1, 1, 2, 2, 2) + (4,) * 14
-LN_GROUPS = (8, 8, 8, 8, 8, 6, 5, 4, 3, 3, 3)
-NZ = 24
+LN_GROUPS = (8, 8, 8, 8, 8, 6, 6, 4, 4, 2, 2)
+NZ = 12
 
 
 def spans(sizes):
@@ -202,7 +202,7 @@ def tile_transducer_kernel(
 
         q_of, q_lo = spans(QUANT_GROUPS)
         g_of, g_lo = spans(LN_GROUPS)
-        pre_of, hid_of, hc_of, lg_of, z_of, stat = {}, {}, {}, {}, {}, {}
+        pre_of, hid_of, hc_of, lg_of, z_of, stat, zpair = {}, {}, {}, {}, {}, {}, {}
 
         def get_stat(k):
             if k not in stat:
@@ -286,8 +286,11 @@ def tile_transducer_kernel(
                 )
 
         def st_e(i, h):
-            if h == 0:
-                z_of[i] = z_pool.tile([P, VOCAB], F32, name="z%d" % i, tag="z")
+            if h == 0 and i % 2 == 0:
+                zz2 = z_pool.tile([P, 2, VOCAB], F32, name="z%d" % i, tag="z")
+                zpair[i // 2] = zz2
+                z_of[i] = zz2[:, 0, :]
+                z_of[i + 1] = zz2[:, 1, :]
             nc.vector.tensor_tensor(
                 out=z_of[i][:, 512 * h : 512 * h + 512],
                 in0=lg_of[i][h][:],
@@ -295,11 +298,12 @@ def tile_transducer_kernel(
                 op=ALU.add,
             )
 
-        def st_m(i):
+        def st_m(s):
+            i = 2 * s
             c = i - g_lo[g_of[i]]
             nc.vector.tensor_reduce(
-                out=get_stat(g_of[i])[0][:, c : c + 1],
-                in_=z_of[i][:],
+                out=get_stat(g_of[i])[0][:, c : c + 2],
+                in_=zpair[s][:],
                 axis=AX.X,
                 op=ALU.max,
                 negate=True,
@@ -311,7 +315,7 @@ def tile_transducer_kernel(
             junk = junk_pool.tile([P, VOCAB], BF16, name="junk%d" % i, tag="junk")
             nc.scalar.activation(
                 out=junk[:],
-                in_=z_of[i][:],
+                in_=z_of[i],
                 func=ACTF.Exp,
                 bias=negm[:, c : c + 1],
                 scale=1.0,
@@ -361,55 +365,65 @@ def tile_transducer_kernel(
                     final_part("pool", i, 640, 1024)
                 else:
                     final_part("pool", i, 0, 1024)
-                nc.sync.dma_start(out=out_rows[P * i : P * i + P, :], in_=z_of[i][:])
+                if i % 2 == 1:
+                    nc.sync.dma_start(
+                        out=out_rows[P * (i - 1) : P * (i + 1), :].rearrange("(a p) v -> p a v", a=2),
+                        in_=zpair[i // 2][:],
+                    )
 
-        def front(i):
-            return min(NT - 1, i + min(RUN_AHEAD, 1 + i))
+        def front(s):
+            return min(NT - 1, 2 * s + 1 + min(RUN_AHEAD, 2 * s))
 
         nxt = {"a": 0, "b": 0, "add": 0, "q": 0}
         q_step = {}
         waiting = []
-        for i in range(NT + 4):
+        for s in range(NT // 2 + 3):
             for b in range(1, NB):
-                if i == TPB * b - RUN_AHEAD - 6:
+                if 2 * s == TPB * b - RUN_AHEAD - 6:
                     project(b)
-                if i == TPB * b - RUN_AHEAD - 5:
+                if 2 * s == TPB * b - RUN_AHEAD - 4:
                     project_out(b)
-            while nxt["a"] <= min(NT - 1, front(i) + (0 if i == 0 else 1)):
+            while nxt["a"] <= min(NT - 1, front(s) + (0 if s == 0 else 1)):
                 if nxt["a"] not in POOL_TILES:
                     st_a(nxt["a"])
                 if nxt["a"] == 0:
                     tables_pe()
                 nxt["a"] += 1
-            while nxt["b"] <= front(i) and nxt["b"] < NT:
+            while nxt["b"] <= front(s) and nxt["b"] < NT:
                 t = nxt["b"]
-                while nxt["add"] < len(POOL_TILES) and POOL_TILES[nxt["add"]] <= front(i) + 3 and t > 0:
+                while nxt["add"] < len(POOL_TILES) and POOL_TILES[nxt["add"]] <= front(s) + 3 and t > 0:
                     st_add(POOL_TILES[nxt["add"]])
                     nxt["add"] += 1
                 st_b(t)
                 if t == 0:
                     tables_out()
                 if t + 1 == NT or q_of[t + 1] != q_of[t]:
-                    q_step[q_of[t]] = i
+                    q_step[q_of[t]] = s
                 nxt["b"] += 1
-            while nxt["q"] in q_step and (q_step[nxt["q"]] < i or q_lo[nxt["q"]] <= i):
+            while nxt["q"] in q_step and q_lo[nxt["q"]] <= 2 * s + 1:
                 st_c(nxt["q"])
                 nxt["q"] += 1
-            if i < NT:
-                st_d(i)
-                st_e(i, 0)
-            if 1 <= i <= NT:
-                st_m(i - 1)
-            if i < NT:
-                st_e(i, 1)
-            while waiting and (waiting[0][1] <= i or i >= NT):
+            if 2 * s < NT:
+                st_d(2 * s)
+                st_d(2 * s + 1)
+                st_e(2 * s, 0)
+                st_e(2 * s, 1)
+            if 1 <= s <= NT // 2:
+                st_m(s - 1)
+            if 2 * s < NT:
+                st_e(2 * s + 1, 0)
+                st_e(2 * s + 1, 1)
+            while nxt["q"] in q_step:
+                st_c(nxt["q"])
+                nxt["q"] += 1
+            while waiting and (waiting[0][1] <= s or 2 * s >= NT):
                 k = waiting.pop(0)[0]
                 st_negc(k)
-                finals(k, i >= NT)
-            t = i - 2
-            if 0 <= t < NT:
-                st_g(t)
-                if t + 1 == NT or g_of[t + 1] != g_of[t]:
-                    st_ln(g_of[t])
-                    waiting.append((g_of[t], i + 1))
+                finals(k, 2 * s >= NT)
+            for t in (2 * s - 2, 2 * s - 1):
+                if 0 <= t < NT:
+                    st_g(t)
+                    if t + 1 == NT or g_of[t + 1] != g_of[t]:
+                        st_ln(g_of[t])
+                        waiting.append((g_of[t], s + 1))
         assert not waiting

@@ -22,10 +22,11 @@ FLOPS = 2 * NB * NTE * NU * INNER * VOCAB + 2 * NB * (NTE + NU) * NH * INNER
 
 MANUAL = True
 RUN_AHEAD = 8
-POOL_TILES = tuple(range(3, 16))
+ADD_LEAD = 9
+POOL_TILES = tuple(range(2, NT, 3))
 QUANT_GROUPS = (1, 1, 2, 2, 2) + (4,) * 14
-LN_GROUPS = (8, 8, 8, 8, 8, 6, 6, 4, 4, 2, 2)
-NZ = 12
+LN_GROUPS = (8, 8, 8, 8, 8, 8, 6, 5, 3, 2)
+NZ = 24
 
 
 def spans(sizes):
@@ -182,27 +183,29 @@ def tile_transducer_kernel(
         project(0)
         project_out(0)
 
-        ptab = const.tile([P, P, 4], F32, name="ptab")
-        dtab = const.tile([P, NU, 4], F32, name="dtab")
+        ptab = [const.tile([P, P, 4], F32, name="ptab%d" % b) for b in range(NB)]
+        dtab = [const.tile([P, NU, 4], F32, name="dtab%d" % b) for b in range(NB)]
+        tab_done = set()
 
-        def tables_pe():
-            pt = ps_pre.tile([P, 4, P], F32, name="pt", tag="pre")
-            hold["pt"] = pt
+        def tables_pe(b):
+            pt = ps_pre.tile([P, 4, P], F32, name="pt%d" % b, tag="pre")
+            hold[b] = pt
             for j in range(4):
-                nc.tensor.transpose(out=pt[:, j, :], in_=pj[0][:, j, :], identity=ident[:])
+                nc.tensor.transpose(out=pt[:, j, :], in_=pj[b][:, j, :], identity=ident[:])
 
-        def tables_out():
-            nc.scalar.copy(out=ptab[:], in_=hold["pt"][:].rearrange("p j c -> p c j"))
+        def tables_out(b):
+            nc.scalar.copy(out=ptab[b][:], in_=hold[b][:].rearrange("p j c -> p c j"))
             nc.gpsimd.tensor_tensor(
-                out=dtab[:],
-                in0=ptab[:, 64:96, :],
-                in1=ptab[:, 96:97, :].to_broadcast([P, NU, 4]),
+                out=dtab[b][:],
+                in0=ptab[b][:, 64:96, :],
+                in1=ptab[b][:, 96:97, :].to_broadcast([P, NU, 4]),
                 op=ALU.add,
             )
+            tab_done.add(b)
 
         q_of, q_lo = spans(QUANT_GROUPS)
         g_of, g_lo = spans(LN_GROUPS)
-        pre_of, hid_of, hc_of, lg_of, z_of, stat, zpair = {}, {}, {}, {}, {}, {}, {}
+        pre_of, hid_of, hc_of, lg_of, z_of, stat = {}, {}, {}, {}, {}, {}
 
         def get_stat(k):
             if k not in stat:
@@ -215,27 +218,30 @@ def tile_transducer_kernel(
             return stat[k]
 
         def st_add(i):
+            b, ti = i // TPB, i % TPB
             pre = add_pool.tile([P, 4, NU, 4], F32, name="apre%d" % i, tag="apre")
             pre_of[i] = pre
             nc.gpsimd.tensor_tensor(
                 out=pre[:],
-                in0=ptab[:, 4 * i : 4 * i + 4, :].unsqueeze(2).to_broadcast([P, 4, NU, 4]),
-                in1=dtab[:].unsqueeze(1).to_broadcast([P, 4, NU, 4]),
+                in0=ptab[b][:, 4 * ti : 4 * ti + 4, :].unsqueeze(2).to_broadcast([P, 4, NU, 4]),
+                in1=dtab[b][:].unsqueeze(1).to_broadcast([P, 4, NU, 4]),
                 op=ALU.add,
             )
 
-        def st_a(i):
-            b, ti = i // TPB, i % TPB
-            pre = ps_pre.tile([P, 4, P], F32, name="pre%d" % i, tag="pre")
-            pre_of[i] = pre
+        def st_a(tiles):
+            b = tiles[0] // TPB
+            for i in tiles:
+                pre_of[i] = ps_pre.tile([P, 4, P], F32, name="pre%d" % i, tag="pre")
             for j in range(4):
-                nc.tensor.matmul(
-                    out=pre[:, j, :],
-                    lhsT=pj[b][:, j, :],
-                    rhs=sel2[:, P * ti : P * ti + P],
-                    start=True,
-                    stop=True,
-                )
+                for i in tiles:
+                    ti = i % TPB
+                    nc.tensor.matmul(
+                        out=pre_of[i][:, j, :],
+                        lhsT=pj[b][:, j, :],
+                        rhs=sel2[:, P * ti : P * ti + P],
+                        start=True,
+                        stop=True,
+                    )
 
         def st_b(i):
             q = q_of[i]
@@ -286,11 +292,8 @@ def tile_transducer_kernel(
                 )
 
         def st_e(i, h):
-            if h == 0 and i % 2 == 0:
-                zz2 = z_pool.tile([P, 2, VOCAB], F32, name="z%d" % i, tag="z")
-                zpair[i // 2] = zz2
-                z_of[i] = zz2[:, 0, :]
-                z_of[i + 1] = zz2[:, 1, :]
+            if h == 0:
+                z_of[i] = z_pool.tile([P, VOCAB], F32, name="z%d" % i, tag="z")
             nc.vector.tensor_tensor(
                 out=z_of[i][:, 512 * h : 512 * h + 512],
                 in0=lg_of[i][h][:],
@@ -298,12 +301,11 @@ def tile_transducer_kernel(
                 op=ALU.add,
             )
 
-        def st_m(s):
-            i = 2 * s
+        def st_m(i):
             c = i - g_lo[g_of[i]]
             nc.vector.tensor_reduce(
-                out=get_stat(g_of[i])[0][:, c : c + 2],
-                in_=zpair[s][:],
+                out=get_stat(g_of[i])[0][:, c : c + 1],
+                in_=z_of[i][:],
                 axis=AX.X,
                 op=ALU.max,
                 negate=True,
@@ -315,7 +317,7 @@ def tile_transducer_kernel(
             junk = junk_pool.tile([P, VOCAB], BF16, name="junk%d" % i, tag="junk")
             nc.scalar.activation(
                 out=junk[:],
-                in_=z_of[i],
+                in_=z_of[i][:],
                 func=ACTF.Exp,
                 bias=negm[:, c : c + 1],
                 scale=1.0,
@@ -354,8 +356,9 @@ def tile_transducer_kernel(
                     op1=ALU.add,
                 )
 
-        def finals(k, late):
-            for i in range(g_lo[k], g_lo[k] + LN_GROUPS[k]):
+        def final_tile(i, late):
+            k = g_of[i]
+            if True:
                 if k == len(LN_GROUPS) - 1:
                     final_part("dve", i, 0, 512)
                     final_part("act", i, 512, 768)
@@ -365,65 +368,74 @@ def tile_transducer_kernel(
                     final_part("pool", i, 640, 1024)
                 else:
                     final_part("pool", i, 0, 1024)
-                if i % 2 == 1:
-                    nc.sync.dma_start(
-                        out=out_rows[P * (i - 1) : P * (i + 1), :].rearrange("(a p) v -> p a v", a=2),
-                        in_=zpair[i // 2][:],
-                    )
+                nc.sync.dma_start(out=out_rows[P * i : P * i + P, :], in_=z_of[i][:])
 
-        def front(s):
-            return min(NT - 1, 2 * s + 1 + min(RUN_AHEAD, 2 * s))
+        def front(i):
+            return min(NT - 1, i + min(RUN_AHEAD, 1 + i))
 
+        a_runs = []
+        for t in range(NT):
+            if t in POOL_TILES:
+                continue
+            if t > 2 and a_runs[-1][-1] == t - 1 and len(a_runs[-1]) < 2 and (t - 1) // TPB == t // TPB:
+                a_runs[-1].append(t)
+            else:
+                a_runs.append([t])
         nxt = {"a": 0, "b": 0, "add": 0, "q": 0}
         q_step = {}
         waiting = []
-        for s in range(NT // 2 + 3):
-            for b in range(1, NB):
-                if 2 * s == TPB * b - RUN_AHEAD - 6:
-                    project(b)
-                if 2 * s == TPB * b - RUN_AHEAD - 4:
-                    project_out(b)
-            while nxt["a"] <= min(NT - 1, front(s) + (0 if s == 0 else 1)):
-                if nxt["a"] not in POOL_TILES:
-                    st_a(nxt["a"])
+        fin_q = []
+        for i in range(NT + 4):
+            while nxt["a"] < len(a_runs) and a_runs[nxt["a"]][0] <= front(i) + (0 if i == 0 else 1):
+                st_a(a_runs[nxt["a"]])
                 if nxt["a"] == 0:
-                    tables_pe()
+                    tables_pe(0)
                 nxt["a"] += 1
-            while nxt["b"] <= front(s) and nxt["b"] < NT:
+            while nxt["b"] <= front(i) and nxt["b"] < NT:
                 t = nxt["b"]
-                while nxt["add"] < len(POOL_TILES) and POOL_TILES[nxt["add"]] <= front(s) + 3 and t > 0:
+                while (
+                    nxt["add"] < len(POOL_TILES)
+                    and POOL_TILES[nxt["add"]] <= front(i) + ADD_LEAD
+                    and POOL_TILES[nxt["add"]] // TPB in tab_done
+                ):
                     st_add(POOL_TILES[nxt["add"]])
                     nxt["add"] += 1
                 st_b(t)
                 if t == 0:
-                    tables_out()
+                    tables_out(0)
                 if t + 1 == NT or q_of[t + 1] != q_of[t]:
-                    q_step[q_of[t]] = s
+                    q_step[q_of[t]] = i
                 nxt["b"] += 1
-            while nxt["q"] in q_step and q_lo[nxt["q"]] <= 2 * s + 1:
+            while nxt["q"] in q_step and (q_step[nxt["q"]] < i or q_lo[nxt["q"]] <= i):
                 st_c(nxt["q"])
                 nxt["q"] += 1
-            if 2 * s < NT:
-                st_d(2 * s)
-                st_d(2 * s + 1)
-                st_e(2 * s, 0)
-                st_e(2 * s, 1)
-            if 1 <= s <= NT // 2:
-                st_m(s - 1)
-            if 2 * s < NT:
-                st_e(2 * s + 1, 0)
-                st_e(2 * s + 1, 1)
-            while nxt["q"] in q_step:
-                st_c(nxt["q"])
-                nxt["q"] += 1
-            while waiting and (waiting[0][1] <= s or 2 * s >= NT):
+            if i < NT:
+                st_d(i)
+                st_e(i, 0)
+            if 1 <= i <= NT:
+                st_m(i - 1)
+            if i < NT:
+                st_e(i, 1)
+            while waiting and (waiting[0][1] <= i or i >= NT):
                 k = waiting.pop(0)[0]
                 st_negc(k)
-                finals(k, 2 * s >= NT)
-            for t in (2 * s - 2, 2 * s - 1):
-                if 0 <= t < NT:
-                    st_g(t)
-                    if t + 1 == NT or g_of[t + 1] != g_of[t]:
-                        st_ln(g_of[t])
-                        waiting.append((g_of[t], s + 1))
-        assert not waiting
+                fin_q.extend(range(g_lo[k], g_lo[k] + LN_GROUPS[k]))
+            for n_f in range(len(fin_q) if i >= NT else min(2, len(fin_q))):
+                final_tile(fin_q.pop(0), i >= NT)
+            for b in range(1, NB):
+                first = max(1, TPB * b - RUN_AHEAD - ADD_LEAD - 4)
+                if i == first:
+                    project(b)
+                if i == first + 1:
+                    project_out(b)
+                if i == first + 2:
+                    tables_pe(b)
+                if i == first + 3:
+                    tables_out(b)
+            t = i - 2
+            if 0 <= t < NT:
+                st_g(t)
+                if t + 1 == NT or g_of[t + 1] != g_of[t]:
+                    st_ln(g_of[t])
+                    waiting.append((g_of[t], i + 1))
+        assert not waiting and not fin_q

@@ -22,11 +22,10 @@ FLOPS = 2 * NB * NTE * NU * INNER * VOCAB + 2 * NB * (NTE + NU) * NH * INNER
 
 MANUAL = True
 RUN_AHEAD = 8
-ADD_LEAD = 9
-POOL_TILES = tuple(range(2, NT, 3))
+POOL_TILES = tuple(range(3, 16))
 QUANT_GROUPS = (1, 1, 2, 2, 2) + (4,) * 14
-LN_GROUPS = (8, 8, 8, 8, 8, 8, 6, 5, 3, 2)
-NZ = 24
+LN_GROUPS = (12, 12, 12, 10, 8, 5, 3, 2)
+NZ = 30
 
 
 def spans(sizes):
@@ -67,6 +66,26 @@ def tile_transducer_kernel(
         warm2 = const.tile([P, 1], F32, name="warm2")
         nc.scalar.activation(out=warm2[:], in_=warm[:], func=ACTF.Exp)
 
+        wzb = const.tile([P, 2048], BF16, name="wzb", align_bytes=64)
+        nc.vector.memset(wzb[:].bitcast(I32), 0)
+        wz = const.tile([P, 512], U32, name="wz", align_bytes=64)
+        wzs = const.tile([P, 512], U8, name="wzs", align_bytes=64)
+        nc.vector.quantize_mx(out=wz[:].bitcast(FP8X4), scales=wzs[:], in_=wzb[:])
+        wps = ps_lg.tile([P, 512], F32, name="wps", tag="lg")
+
+        def keep_warm(count):
+            for n_w in range(count):
+                nc.tensor.matmul_mx(
+                    out=wps[:],
+                    lhsT=wz[:, 0:P].bitcast(FP8X4),
+                    lhsT_scale=wzs[:, 0:P],
+                    rhs=wz[:].bitcast(FP8X4),
+                    rhs_scale=wzs[:],
+                    start=True,
+                    stop=True,
+                )
+
+        keep_warm(3)
         w1s = const.tile([P, 2, INNER], U8, name="w1s", align_bytes=64)
         nc.vector.memset(w1s[:].bitcast(I32), 0)
         w2s = const.tile([P, VOCAB], U8, name="w2s", align_bytes=64)
@@ -126,6 +145,7 @@ def tile_transducer_kernel(
             nc.tensor.transpose(out=xtd[:, u, :], in_=xdw[:, u:256:2], identity=ident[:])
         for u in range(2):
             nc.tensor.transpose(out=xt1[:, u, :], in_=xew[:, 1, u:256:2], identity=ident[:])
+        keep_warm(5)
         nc.vector.tensor_copy(
             out=gxw[:, 0:4:2, 0:NTE, :], in_=xt0[:].rearrange("p u (b t) -> p b t u", b=2)
         )
@@ -181,27 +201,26 @@ def tile_transducer_kernel(
             )
 
         project(0)
+        keep_warm(2)
         project_out(0)
 
-        ptab = [const.tile([P, P, 4], F32, name="ptab%d" % b) for b in range(NB)]
-        dtab = [const.tile([P, NU, 4], F32, name="dtab%d" % b) for b in range(NB)]
-        tab_done = set()
+        ptab = const.tile([P, P, 4], F32, name="ptab")
+        dtab = const.tile([P, NU, 4], F32, name="dtab")
 
-        def tables_pe(b):
-            pt = ps_pre.tile([P, 4, P], F32, name="pt%d" % b, tag="pre")
-            hold[b] = pt
+        def tables_pe():
+            pt = ps_pre.tile([P, 4, P], F32, name="pt", tag="pre")
+            hold["pt"] = pt
             for j in range(4):
-                nc.tensor.transpose(out=pt[:, j, :], in_=pj[b][:, j, :], identity=ident[:])
+                nc.tensor.transpose(out=pt[:, j, :], in_=pj[0][:, j, :], identity=ident[:])
 
-        def tables_out(b):
-            nc.scalar.copy(out=ptab[b][:], in_=hold[b][:].rearrange("p j c -> p c j"))
+        def tables_out():
+            nc.scalar.copy(out=ptab[:], in_=hold["pt"][:].rearrange("p j c -> p c j"))
             nc.gpsimd.tensor_tensor(
-                out=dtab[b][:],
-                in0=ptab[b][:, 64:96, :],
-                in1=ptab[b][:, 96:97, :].to_broadcast([P, NU, 4]),
+                out=dtab[:],
+                in0=ptab[:, 64:96, :],
+                in1=ptab[:, 96:97, :].to_broadcast([P, NU, 4]),
                 op=ALU.add,
             )
-            tab_done.add(b)
 
         q_of, q_lo = spans(QUANT_GROUPS)
         g_of, g_lo = spans(LN_GROUPS)
@@ -210,38 +229,35 @@ def tile_transducer_kernel(
         def get_stat(k):
             if k not in stat:
                 stat[k] = (
-                    stat_pool.tile([P, 8], F32, name="negm%d" % k, tag="negm"),
-                    stat_pool.tile([P, 8], F32, name="ssum%d" % k, tag="ssum"),
-                    stat_pool.tile([P, 8], F32, name="lns%d" % k, tag="lns"),
-                    stat_pool.tile([P, 8], F32, name="negc%d" % k, tag="negc"),
+                    stat_pool.tile([P, 16], F32, name="negm%d" % k, tag="negm"),
+                    stat_pool.tile([P, 16], F32, name="ssum%d" % k, tag="ssum"),
+                    stat_pool.tile([P, 16], F32, name="lns%d" % k, tag="lns"),
+                    stat_pool.tile([P, 16], F32, name="negc%d" % k, tag="negc"),
                 )
             return stat[k]
 
         def st_add(i):
-            b, ti = i // TPB, i % TPB
             pre = add_pool.tile([P, 4, NU, 4], F32, name="apre%d" % i, tag="apre")
             pre_of[i] = pre
             nc.gpsimd.tensor_tensor(
                 out=pre[:],
-                in0=ptab[b][:, 4 * ti : 4 * ti + 4, :].unsqueeze(2).to_broadcast([P, 4, NU, 4]),
-                in1=dtab[b][:].unsqueeze(1).to_broadcast([P, 4, NU, 4]),
+                in0=ptab[:, 4 * i : 4 * i + 4, :].unsqueeze(2).to_broadcast([P, 4, NU, 4]),
+                in1=dtab[:].unsqueeze(1).to_broadcast([P, 4, NU, 4]),
                 op=ALU.add,
             )
 
-        def st_a(tiles):
-            b = tiles[0] // TPB
-            for i in tiles:
-                pre_of[i] = ps_pre.tile([P, 4, P], F32, name="pre%d" % i, tag="pre")
+        def st_a(i):
+            b, ti = i // TPB, i % TPB
+            pre = ps_pre.tile([P, 4, P], F32, name="pre%d" % i, tag="pre")
+            pre_of[i] = pre
             for j in range(4):
-                for i in tiles:
-                    ti = i % TPB
-                    nc.tensor.matmul(
-                        out=pre_of[i][:, j, :],
-                        lhsT=pj[b][:, j, :],
-                        rhs=sel2[:, P * ti : P * ti + P],
-                        start=True,
-                        stop=True,
-                    )
+                nc.tensor.matmul(
+                    out=pre[:, j, :],
+                    lhsT=pj[b][:, j, :],
+                    rhs=sel2[:, P * ti : P * ti + P],
+                    start=True,
+                    stop=True,
+                )
 
         def st_b(i):
             q = q_of[i]
@@ -356,9 +372,8 @@ def tile_transducer_kernel(
                     op1=ALU.add,
                 )
 
-        def final_tile(i, late):
-            k = g_of[i]
-            if True:
+        def finals(k, late):
+            for i in range(g_lo[k], g_lo[k] + LN_GROUPS[k]):
                 if k == len(LN_GROUPS) - 1:
                     final_part("dve", i, 0, 512)
                     final_part("act", i, 512, 768)
@@ -373,36 +388,29 @@ def tile_transducer_kernel(
         def front(i):
             return min(NT - 1, i + min(RUN_AHEAD, 1 + i))
 
-        a_runs = []
-        for t in range(NT):
-            if t in POOL_TILES:
-                continue
-            if t > 2 and a_runs[-1][-1] == t - 1 and len(a_runs[-1]) < 2 and (t - 1) // TPB == t // TPB:
-                a_runs[-1].append(t)
-            else:
-                a_runs.append([t])
         nxt = {"a": 0, "b": 0, "add": 0, "q": 0}
         q_step = {}
         waiting = []
-        fin_q = []
         for i in range(NT + 4):
-            while nxt["a"] < len(a_runs) and a_runs[nxt["a"]][0] <= front(i) + (0 if i == 0 else 1):
-                st_a(a_runs[nxt["a"]])
+            for b in range(1, NB):
+                if i == TPB * b - RUN_AHEAD - 6:
+                    project(b)
+                if i == TPB * b - RUN_AHEAD - 5:
+                    project_out(b)
+            while nxt["a"] <= min(NT - 1, front(i) + (0 if i == 0 else 1)):
+                if nxt["a"] not in POOL_TILES:
+                    st_a(nxt["a"])
                 if nxt["a"] == 0:
-                    tables_pe(0)
+                    tables_pe()
                 nxt["a"] += 1
             while nxt["b"] <= front(i) and nxt["b"] < NT:
                 t = nxt["b"]
-                while (
-                    nxt["add"] < len(POOL_TILES)
-                    and POOL_TILES[nxt["add"]] <= front(i) + ADD_LEAD
-                    and POOL_TILES[nxt["add"]] // TPB in tab_done
-                ):
+                while nxt["add"] < len(POOL_TILES) and POOL_TILES[nxt["add"]] <= front(i) + 3 and t > 0:
                     st_add(POOL_TILES[nxt["add"]])
                     nxt["add"] += 1
                 st_b(t)
                 if t == 0:
-                    tables_out(0)
+                    tables_out()
                 if t + 1 == NT or q_of[t + 1] != q_of[t]:
                     q_step[q_of[t]] = i
                 nxt["b"] += 1
@@ -419,23 +427,11 @@ def tile_transducer_kernel(
             while waiting and (waiting[0][1] <= i or i >= NT):
                 k = waiting.pop(0)[0]
                 st_negc(k)
-                fin_q.extend(range(g_lo[k], g_lo[k] + LN_GROUPS[k]))
-            for n_f in range(len(fin_q) if i >= NT else min(2, len(fin_q))):
-                final_tile(fin_q.pop(0), i >= NT)
-            for b in range(1, NB):
-                first = max(1, TPB * b - RUN_AHEAD - ADD_LEAD - 4)
-                if i == first:
-                    project(b)
-                if i == first + 1:
-                    project_out(b)
-                if i == first + 2:
-                    tables_pe(b)
-                if i == first + 3:
-                    tables_out(b)
+                finals(k, i >= NT)
             t = i - 2
             if 0 <= t < NT:
                 st_g(t)
                 if t + 1 == NT or g_of[t + 1] != g_of[t]:
                     st_ln(g_of[t])
                     waiting.append((g_of[t], i + 1))
-        assert not waiting and not fin_q
+        assert not waiting

@@ -66,26 +66,6 @@ def tile_transducer_kernel(
         warm2 = const.tile([P, 1], F32, name="warm2")
         nc.scalar.activation(out=warm2[:], in_=warm[:], func=ACTF.Exp)
 
-        wzb = const.tile([P, 2048], BF16, name="wzb", align_bytes=64)
-        nc.vector.memset(wzb[:].bitcast(I32), 0)
-        wz = const.tile([P, 512], U32, name="wz", align_bytes=64)
-        wzs = const.tile([P, 512], U8, name="wzs", align_bytes=64)
-        nc.vector.quantize_mx(out=wz[:].bitcast(FP8X4), scales=wzs[:], in_=wzb[:])
-        wps = ps_lg.tile([P, 512], F32, name="wps", tag="lg")
-
-        def keep_warm(count):
-            for n_w in range(count):
-                nc.tensor.matmul_mx(
-                    out=wps[:],
-                    lhsT=wz[:, 0:P].bitcast(FP8X4),
-                    lhsT_scale=wzs[:, 0:P],
-                    rhs=wz[:].bitcast(FP8X4),
-                    rhs_scale=wzs[:],
-                    start=True,
-                    stop=True,
-                )
-
-        keep_warm(3)
         w1s = const.tile([P, 2, INNER], U8, name="w1s", align_bytes=64)
         nc.vector.memset(w1s[:].bitcast(I32), 0)
         w2s = const.tile([P, VOCAB], U8, name="w2s", align_bytes=64)
@@ -145,7 +125,6 @@ def tile_transducer_kernel(
             nc.tensor.transpose(out=xtd[:, u, :], in_=xdw[:, u:256:2], identity=ident[:])
         for u in range(2):
             nc.tensor.transpose(out=xt1[:, u, :], in_=xew[:, 1, u:256:2], identity=ident[:])
-        keep_warm(5)
         nc.vector.tensor_copy(
             out=gxw[:, 0:4:2, 0:NTE, :], in_=xt0[:].rearrange("p u (b t) -> p b t u", b=2)
         )
@@ -201,7 +180,6 @@ def tile_transducer_kernel(
             )
 
         project(0)
-        keep_warm(2)
         project_out(0)
 
         ptab = const.tile([P, P, 4], F32, name="ptab")

@@ -24,8 +24,8 @@ MANUAL = True
 RUN_AHEAD = 8
 POOL_TILES = tuple(range(3, 16))
 QUANT_GROUPS = (1, 1, 2, 2, 2) + (4,) * 14
-LN_GROUPS = (12, 12, 12, 10, 8, 5, 3, 2)
-NZ = 30
+LN_GROUPS = (18, 16, 12, 8, 5, 3, 2)
+NZ = 32
 
 
 def spans(sizes):
@@ -50,10 +50,10 @@ def tile_transducer_kernel(
         ps_lg = ctx.enter_context(tc.psum_pool(name="ps_lg", bufs=4))
         hid_pool = ctx.enter_context(tc.tile_pool(name="hid", bufs=4))
         hc_pool = ctx.enter_context(tc.tile_pool(name="hc", bufs=4))
-        add_pool = ctx.enter_context(tc.tile_pool(name="addp", bufs=8))
+        add_pool = ctx.enter_context(tc.tile_pool(name="addp", bufs=6))
         z_pool = ctx.enter_context(tc.tile_pool(name="zp", bufs=NZ))
         junk_pool = ctx.enter_context(tc.tile_pool(name="junk", bufs=2))
-        stat_pool = ctx.enter_context(tc.tile_pool(name="stat", bufs=8))
+        stat_pool = ctx.enter_context(tc.tile_pool(name="stat", bufs=6))
 
         warm = const.tile([P, 1], F32, name="warm")
         nc.vector.memset(warm[:], 0.0)
@@ -66,6 +66,26 @@ def tile_transducer_kernel(
         warm2 = const.tile([P, 1], F32, name="warm2")
         nc.scalar.activation(out=warm2[:], in_=warm[:], func=ACTF.Exp)
 
+        wzb = const.tile([P, 2048], BF16, name="wzb", align_bytes=64)
+        nc.vector.memset(wzb[:].bitcast(I32), 0)
+        wz = const.tile([P, 512], U32, name="wz", align_bytes=64)
+        wzs = const.tile([P, 512], U8, name="wzs", align_bytes=64)
+        nc.vector.quantize_mx(out=wz[:].bitcast(FP8X4), scales=wzs[:], in_=wzb[:])
+        wps = ps_lg.tile([P, 512], F32, name="wps", tag="lg")
+
+        def keep_warm(count):
+            for n_w in range(count):
+                nc.tensor.matmul_mx(
+                    out=wps[:],
+                    lhsT=wz[:, 0:P].bitcast(FP8X4),
+                    lhsT_scale=wzs[:, 0:P],
+                    rhs=wz[:].bitcast(FP8X4),
+                    rhs_scale=wzs[:],
+                    start=True,
+                    stop=True,
+                )
+
+        keep_warm(3)
         w1s = const.tile([P, 2, INNER], U8, name="w1s", align_bytes=64)
         nc.vector.memset(w1s[:].bitcast(I32), 0)
         w2s = const.tile([P, VOCAB], U8, name="w2s", align_bytes=64)
@@ -125,6 +145,7 @@ def tile_transducer_kernel(
             nc.tensor.transpose(out=xtd[:, u, :], in_=xdw[:, u:256:2], identity=ident[:])
         for u in range(2):
             nc.tensor.transpose(out=xt1[:, u, :], in_=xew[:, 1, u:256:2], identity=ident[:])
+        keep_warm(5)
         nc.vector.tensor_copy(
             out=gxw[:, 0:4:2, 0:NTE, :], in_=xt0[:].rearrange("p u (b t) -> p b t u", b=2)
         )
@@ -180,6 +201,7 @@ def tile_transducer_kernel(
             )
 
         project(0)
+        keep_warm(2)
         project_out(0)
 
         ptab = const.tile([P, P, 4], F32, name="ptab")
@@ -207,10 +229,10 @@ def tile_transducer_kernel(
         def get_stat(k):
             if k not in stat:
                 stat[k] = (
-                    stat_pool.tile([P, 16], F32, name="negm%d" % k, tag="negm"),
-                    stat_pool.tile([P, 16], F32, name="ssum%d" % k, tag="ssum"),
-                    stat_pool.tile([P, 16], F32, name="lns%d" % k, tag="lns"),
-                    stat_pool.tile([P, 16], F32, name="negc%d" % k, tag="negc"),
+                    stat_pool.tile([P, 24], F32, name="negm%d" % k, tag="negm"),
+                    stat_pool.tile([P, 24], F32, name="ssum%d" % k, tag="ssum"),
+                    stat_pool.tile([P, 24], F32, name="lns%d" % k, tag="lns"),
+                    stat_pool.tile([P, 24], F32, name="negc%d" % k, tag="negc"),
                 )
             return stat[k]
 

from contextlib import ExitStack

import concourse.mybir as mybir
from concourse.masks import make_identity

F32 = mybir.dt.float32
BF16 = mybir.dt.bfloat16
I32 = mybir.dt.int32
U32 = mybir.dt.uint32
U8 = mybir.dt.uint8
FP8X4 = mybir.dt.float8_e4m3fn_x4
ALU = mybir.AluOpType
ACTF = mybir.ActivationFunctionType
AX = mybir.AxisListType

P = 128
NB, NTE, NU, NH = 4, 64, 32, 512
INNER, VOCAB = 512, 1024
NT = NB * NTE * NU // P
TPB = NT // NB
FLOPS = 2 * NB * NTE * NU * INNER * VOCAB + 2 * NB * (NTE + NU) * NH * INNER

MANUAL = True
RUN_AHEAD = 8
POOL_TILES = tuple(range(3, 16))
QUANT_GROUPS = (1, 1, 2, 2, 2) + (4,) * 14
LN_GROUPS = (18, 16, 12, 8, 5, 3, 2)
NZ = 32


def spans(sizes):
    of, lo = [], []
    for k, n_k in enumerate(sizes):
        lo.append(len(of))
        of.extend([k] * n_k)
    assert len(of) == NT
    return of, lo


def tile_transducer_kernel(
    tc, enc_state, dec_state, W1_words, W1_scales, b1, W2_words, W2_scales, b2, out
):
    nc = tc.nc
    out_rows = out.flatten_outer_dims()
    with ExitStack() as ctx:
        if MANUAL:
            ctx.enter_context(tc.manual_schedule())
        const = ctx.enter_context(tc.tile_pool(name="const", bufs=1))
        ps_pre = ctx.enter_context(tc.psum_pool(name="ps_pre", bufs=4))
        ps_lg = ctx.enter_context(tc.psum_pool(name="ps_lg", bufs=4))
        hid_pool = ctx.enter_context(tc.tile_pool(name="hid", bufs=4))
        hc_pool = ctx.enter_context(tc.tile_pool(name="hc", bufs=4))
        add_pool = ctx.enter_context(tc.tile_pool(name="addp", bufs=6))
        z_pool = ctx.enter_context(tc.tile_pool(name="zp", bufs=NZ))
        junk_pool = ctx.enter_context(tc.tile_pool(name="junk", bufs=2))
        stat_pool = ctx.enter_context(tc.tile_pool(name="stat", bufs=6))

        warm = const.tile([P, 1], F32, name="warm")
        nc.vector.memset(warm[:], 0.0)
        xe = const.tile([P, 2, NH], BF16, name="xe", align_bytes=64)
        nc.scalar.dma_start(
            out=xe[:], in_=enc_state.flatten_outer_dims().rearrange("(e p) k -> p e k", p=P)
        )
        xd = const.tile([P, NH], BF16, name="xd", align_bytes=64)
        nc.scalar.dma_start(out=xd[:], in_=dec_state.flatten_outer_dims())
        warm2 = const.tile([P, 1], F32, name="warm2")
        nc.scalar.activation(out=warm2[:], in_=warm[:], func=ACTF.Exp)

        wzb = const.tile([P, 2048], BF16, name="wzb", align_bytes=64)
        nc.vector.memset(wzb[:].bitcast(I32), 0)
        wz = const.tile([P, 512], U32, name="wz", align_bytes=64)
        wzs = const.tile([P, 512], U8, name="wzs", align_bytes=64)
        nc.vector.quantize_mx(out=wz[:].bitcast(FP8X4), scales=wzs[:], in_=wzb[:])
        wps = ps_lg.tile([P, 512], F32, name="wps", tag="lg")

        def keep_warm(count):
            for n_w in range(count):
                nc.tensor.matmul_mx(
                    out=wps[:],
                    lhsT=wz[:, 0:P].bitcast(FP8X4),
                    lhsT_scale=wzs[:, 0:P],
                    rhs=wz[:].bitcast(FP8X4),
                    rhs_scale=wzs[:],
                    start=True,
                    stop=True,
                )

        keep_warm(3)
        w1s = const.tile([P, 2, INNER], U8, name="w1s", align_bytes=64)
        nc.vector.memset(w1s[:].bitcast(I32), 0)
        w2s = const.tile([P, VOCAB], U8, name="w2s", align_bytes=64)
        nc.vector.memset(w2s[:].bitcast(I32), 0)
        b1st = const.tile([P, INNER], BF16, name="b1st", align_bytes=64)
        nc.vector.memset(b1st[:].bitcast(I32), 0)
        gx = const.tile([P, 8, P, 4], BF16, name="gx", align_bytes=64)
        nc.vector.memset(gx[:].bitcast(I32), 0)

        for q in range(4):
            nc.sync.dma_start(
                out=w1s[32 * q : 32 * q + 4, :, :].bitcast(I32),
                in_=W1_scales[:, 4 * q : 4 * q + 4, :].rearrange("g r n -> r g n").bitcast(I32),
            )
        w1w = const.tile([P, 2, INNER], U32, name="w1w", align_bytes=64)
        nc.sync.dma_start(
            out=w1w[:].bitcast(I32),
            in_=W1_words.rearrange("g p n t -> p g (n t)").bitcast(I32),
        )
        nc.sync.dma_start(out=b1st[96:97, :], in_=b1.unsqueeze(0))
        for q in range(4):
            nc.sync.dma_start(
                out=w2s[32 * q : 32 * q + 4, :].bitcast(I32),
                in_=W2_scales[0, 4 * q : 4 * q + 4, :].bitcast(I32),
            )
        w2w = const.tile([P, VOCAB], U32, name="w2w", align_bytes=64)
        nc.sync.dma_start(
            out=w2w[:].bitcast(I32), in_=W2_words[0].rearrange("p n t -> p (n t)").bitcast(I32)
        )
        b2bc = const.tile([P, VOCAB], BF16, name="b2bc")
        nc.scalar.dma_start(out=b2bc[:], in_=b2.partition_broadcast(P))

        ident = const.tile([P, P], F32, name="ident")
        make_identity(nc, ident[:])
        usel = const.tile([P, NU], F32, name="usel")
        nc.vector.tensor_scalar(
            out=usel[:], in0=ident[:, 64:96], scalar1=ident[:, 96:97], scalar2=None, op0=ALU.add
        )
        sel = const.tile([P, NTE, NU], F32, name="sel")
        nc.vector.tensor_tensor(
            out=sel[:],
            in0=ident[:, 0:NTE].unsqueeze(2).to_broadcast([P, NTE, NU]),
            in1=usel[:].unsqueeze(1).to_broadcast([P, NTE, NU]),
            op=ALU.add,
        )
        sel2 = sel[:].rearrange("c t u -> c (t u)")

        xew = xe[:].bitcast(F32)
        xdw = xd[:].bitcast(F32)
        gxw = gx[:].bitcast(F32)
        xt0 = ps_pre.tile([P, 2, P], F32, name="xt0", tag="pre")
        xtd = ps_pre.tile([P, 2, P], F32, name="xtd", tag="pre")
        xt1 = ps_pre.tile([P, 2, P], F32, name="xt1", tag="pre")
        for u in range(2):
            nc.tensor.transpose(out=xt0[:, u, :], in_=xew[:, 0, u:256:2], identity=ident[:])
        for u in range(2):
            nc.tensor.transpose(out=xtd[:, u, :], in_=xdw[:, u:256:2], identity=ident[:])
        for u in range(2):
            nc.tensor.transpose(out=xt1[:, u, :], in_=xew[:, 1, u:256:2], identity=ident[:])
        keep_warm(5)
        nc.vector.tensor_copy(
            out=gxw[:, 0:4:2, 0:NTE, :], in_=xt0[:].rearrange("p u (b t) -> p b t u", b=2)
        )
        nc.scalar.copy(
            out=gxw[:, 1:8:2, 64:96, :], in_=xtd[:].rearrange("p u (b v) -> p b v u", b=4)
        )
        nc.scalar.copy(
            out=gxw[:, 4:8:2, 0:NTE, :], in_=xt1[:].rearrange("p u (b t) -> p b t u", b=2)
        )
        cx = const.tile([P, 8, P], U32, name="cx", align_bytes=64)
        sx = const.tile([P, 8, P], U8, name="sx", align_bytes=64)

        def quant_x(s0, ns):
            nc.vector.quantize_mx(
                out=cx[:, s0 : s0 + ns, :].rearrange("p s c -> p (s c)").bitcast(FP8X4),
                scales=sx[:, s0 : s0 + ns, :].rearrange("p s c -> p (s c)"),
                in_=gx[:, s0 : s0 + ns, :, :].rearrange("p s c t -> p (s c t)"),
            )

        pj = [const.tile([P, 4, P], F32, name="pj%d" % b) for b in range(NB)]

        def bias_rows(b):
            nc.vector.tensor_copy(
                out=pj[b][96:128, :, :], in_=b1st[96:128, :].rearrange("c (p j) -> c j p", j=4)
            )

        quant_x(0, 2)
        bias_rows(0)
        quant_x(2, 2)
        quant_x(4, 4)
        for b in range(1, NB):
            bias_rows(b)

        hold = {}

        def project(b):
            pp = ps_pre.tile([P, INNER], F32, name="pp%d" % b, tag="pre")
            hold[b] = pp
            for g in range(2):
                nc.tensor.matmul_mx(
                    out=pp[:],
                    lhsT=cx[:, 2 * b + g, :].bitcast(FP8X4),
                    lhsT_scale=sx[:, 2 * b + g, :],
                    rhs=w1w[:, g, :].bitcast(FP8X4),
                    rhs_scale=w1s[:, g, :],
                    start=(g == 0),
                    stop=(g == 1),
                )

        def project_out(b):
            nc.scalar.copy(
                out=pj[b][0:96, :, :], in_=hold[b][0:96, :].rearrange("c (p j) -> c j p", j=4)
            )

        project(0)
        keep_warm(2)
        project_out(0)

        ptab = const.tile([P, P, 4], F32, name="ptab")
        dtab = const.tile([P, NU, 4], F32, name="dtab")

        def tables_pe():
            pt = ps_pre.tile([P, 4, P], F32, name="pt", tag="pre")
            hold["pt"] = pt
            for j in range(4):
                nc.tensor.transpose(out=pt[:, j, :], in_=pj[0][:, j, :], identity=ident[:])

        def tables_out():
            nc.scalar.copy(out=ptab[:], in_=hold["pt"][:].rearrange("p j c -> p c j"))
            nc.gpsimd.tensor_tensor(
                out=dtab[:],
                in0=ptab[:, 64:96, :],
                in1=ptab[:, 96:97, :].to_broadcast([P, NU, 4]),
                op=ALU.add,
            )

        q_of, q_lo = spans(QUANT_GROUPS)
        g_of, g_lo = spans(LN_GROUPS)
        pre_of, hid_of, hc_of, lg_of, z_of, stat = {}, {}, {}, {}, {}, {}

        def get_stat(k):
            if k not in stat:
                stat[k] = (
                    stat_pool.tile([P, 24], F32, name="negm%d" % k, tag="negm"),
                    stat_pool.tile([P, 24], F32, name="ssum%d" % k, tag="ssum"),
                    stat_pool.tile([P, 24], F32, name="lns%d" % k, tag="lns"),
                    stat_pool.tile([P, 24], F32, name="negc%d" % k, tag="negc"),
                )
            return stat[k]

        def st_add(i):
            pre = add_pool.tile([P, 4, NU, 4], F32, name="apre%d" % i, tag="apre")
            pre_of[i] = pre
            nc.gpsimd.tensor_tensor(
                out=pre[:],
                in0=ptab[:, 4 * i : 4 * i + 4, :].unsqueeze(2).to_broadcast([P, 4, NU, 4]),
                in1=dtab[:].unsqueeze(1).to_broadcast([P, 4, NU, 4]),
                op=ALU.add,
            )

        def st_a(i):
            b, ti = i // TPB, i % TPB
            pre = ps_pre.tile([P, 4, P], F32, name="pre%d" % i, tag="pre")
            pre_of[i] = pre
            for j in range(4):
                nc.tensor.matmul(
                    out=pre[:, j, :],
                    lhsT=pj[b][:, j, :],
                    rhs=sel2[:, P * ti : P * ti + P],
                    start=True,
                    stop=True,
                )

        def st_b(i):
            q = q_of[i]
            pos = i - q_lo[q]
            if pos == 0:
                hid_of[q] = hid_pool.tile(
                    [P, QUANT_GROUPS[q] * P, 4], BF16, name="hid%d" % q, tag="hid", align_bytes=64
                )
            dst = hid_of[q][:, P * pos : P * pos + P, :]
            if i in POOL_TILES:
                nc.scalar.activation(
                    out=dst.rearrange("p r j -> p (r j)"),
                    in_=pre_of[i][:].rearrange("p a u j -> p (a u j)"),
                    func=ACTF.Tanh,
                )
            else:
                nc.scalar.activation(
                    out=dst, in_=pre_of[i][:].rearrange("p j r -> p r j"), func=ACTF.Tanh
                )

        def st_c(q):
            n_q = QUANT_GROUPS[q]
            hc = hc_pool.tile([P, n_q * P], U32, name="hc%d" % q, tag="hc", align_bytes=64)
            hs = hc_pool.tile([P, n_q * P], U8, name="hs%d" % q, tag="hs", align_bytes=64)
            hc_of[q] = (hc, hs)
            nc.vector.quantize_mx(
                out=hc[:].bitcast(FP8X4),
                scales=hs[:],
                in_=hid_of[q][:].rearrange("p r j -> p (r j)"),
            )

        def st_d(i):
            q = q_of[i]
            pos = i - q_lo[q]
            hc, hs = hc_of[q]
            lg_of[i] = []
            for h in range(2):
                lg = ps_lg.tile([P, 512], F32, name="lg%d_%d" % (i, h), tag="lg")
                lg_of[i].append(lg)
                nc.tensor.matmul_mx(
                    out=lg[:],
                    lhsT=hc[:, P * pos : P * pos + P].bitcast(FP8X4),
                    lhsT_scale=hs[:, P * pos : P * pos + P],
                    rhs=w2w[:, 512 * h : 512 * h + 512].bitcast(FP8X4),
                    rhs_scale=w2s[:, 512 * h : 512 * h + 512],
                    start=True,
                    stop=True,
                )

        def st_e(i, h):
            if h == 0:
                z_of[i] = z_pool.tile([P, VOCAB], F32, name="z%d" % i, tag="z")
            nc.vector.tensor_tensor(
                out=z_of[i][:, 512 * h : 512 * h + 512],
                in0=lg_of[i][h][:],
                in1=b2bc[:, 512 * h : 512 * h + 512],
                op=ALU.add,
            )

        def st_m(i):
            c = i - g_lo[g_of[i]]
            nc.vector.tensor_reduce(
                out=get_stat(g_of[i])[0][:, c : c + 1],
                in_=z_of[i][:],
                axis=AX.X,
                op=ALU.max,
                negate=True,
            )

        def st_g(i):
            c = i - g_lo[g_of[i]]
            negm, ssum = get_stat(g_of[i])[0], get_stat(g_of[i])[1]
            junk = junk_pool.tile([P, VOCAB], BF16, name="junk%d" % i, tag="junk")
            nc.scalar.activation(
                out=junk[:],
                in_=z_of[i][:],
                func=ACTF.Exp,
                bias=negm[:, c : c + 1],
                scale=1.0,
                accum_out=ssum[:, c : c + 1],
            )

        def st_ln(k):
            n_k = LN_GROUPS[k]
            nc.scalar.activation(
                out=get_stat(k)[2][:, 0:n_k], in_=get_stat(k)[1][:, 0:n_k], func=ACTF.Ln
            )

        def st_negc(k):
            n_k = LN_GROUPS[k]
            negm, ssum, lns, negc = get_stat(k)
            nc.vector.tensor_tensor(
                out=negc[:, 0:n_k], in0=negm[:, 0:n_k], in1=lns[:, 0:n_k], op=ALU.subtract
            )

        def final_part(eng_name, i, lo, hi):
            c = i - g_lo[g_of[i]]
            negc = get_stat(g_of[i])[3]
            zz = z_of[i][:, lo:hi]
            if eng_name == "act":
                nc.scalar.activation(
                    out=zz, in_=zz, func=ACTF.Identity, bias=negc[:, c : c + 1], scale=1.0
                )
            else:
                eng = nc.vector if eng_name == "dve" else nc.gpsimd
                eng.tensor_scalar(
                    out=zz,
                    in0=zz,
                    scalar1=1.0,
                    scalar2=negc[:, c : c + 1],
                    op0=ALU.mult,
                    op1=ALU.add,
                )

        def finals(k, late):
            for i in range(g_lo[k], g_lo[k] + LN_GROUPS[k]):
                if k == len(LN_GROUPS) - 1:
                    final_part("dve", i, 0, 512)
                    final_part("act", i, 512, 768)
                    final_part("pool", i, 768, 1024)
                elif late:
                    final_part("dve", i, 0, 640)
                    final_part("pool", i, 640, 1024)
                else:
                    final_part("pool", i, 0, 1024)
                nc.sync.dma_start(out=out_rows[P * i : P * i + P, :], in_=z_of[i][:])

        def front(i):
            return min(NT - 1, i + min(RUN_AHEAD, 1 + i))

        nxt = {"a": 0, "b": 0, "add": 0, "q": 0}
        q_step = {}
        waiting = []
        for i in range(NT + 4):
            for b in range(1, NB):
                if i == TPB * b - RUN_AHEAD - 6:
                    project(b)
                if i == TPB * b - RUN_AHEAD - 5:
                    project_out(b)
            while nxt["a"] <= min(NT - 1, front(i) + (0 if i == 0 else 1)):
                if nxt["a"] not in POOL_TILES:
                    st_a(nxt["a"])
                if nxt["a"] == 0:
                    tables_pe()
                nxt["a"] += 1
            while nxt["b"] <= front(i) and nxt["b"] < NT:
                t = nxt["b"]
                while nxt["add"] < len(POOL_TILES) and POOL_TILES[nxt["add"]] <= front(i) + 3 and t > 0:
                    st_add(POOL_TILES[nxt["add"]])
                    nxt["add"] += 1
                st_b(t)
                if t == 0:
                    tables_out()
                if t + 1 == NT or q_of[t + 1] != q_of[t]:
                    q_step[q_of[t]] = i
                nxt["b"] += 1
            while nxt["q"] in q_step and (q_step[nxt["q"]] < i or q_lo[nxt["q"]] <= i):
                st_c(nxt["q"])
                nxt["q"] += 1
            if i < NT:
                st_d(i)
                st_e(i, 0)
            if 1 <= i <= NT:
                st_m(i - 1)
            if i < NT:
                st_e(i, 1)
            while waiting and (waiting[0][1] <= i or i >= NT):
                k = waiting.pop(0)[0]
                st_negc(k)
                finals(k, i >= NT)
            t = i - 2
            if 0 <= t < NT:
                st_g(t)
                if t + 1 == NT or g_of[t + 1] != g_of[t]:
                    st_ln(g_of[t])
                    waiting.append((g_of[t], i + 1))
        assert not waiting
